import numpy as np
import ml_dtypes


def mxq(x, axis, fmt="e4m3"):
    dtype, down = {"e4m3": (ml_dtypes.float8_e4m3fn, 7), "e5m2": (ml_dtypes.float8_e5m2, 14)}[fmt]
    v = np.moveaxis(np.asarray(x, np.float32).astype(ml_dtypes.bfloat16).astype(np.float64), axis, -1)
    blocks = v.reshape(v.shape[:-1] + (-1, 32))
    amax = np.abs(blocks).max(-1, keepdims=True)
    byte = np.maximum(np.where(amax > 0, np.frexp(amax)[1] - 1 + 127, 0) - down, 1)
    scale = np.exp2(byte - 127.0)
    codes = (blocks / scale).astype(np.float32).astype(dtype).astype(np.float64)
    return np.moveaxis((codes * scale).reshape(v.shape), -1, axis)


WIDE = False


def mx_kscale(k):
    if not WIDE:
        return np.ones(k)
    levels = np.array([10, -10, 5, -5, 0])
    a = np.random.permutation(np.resize(levels, k // 512 * 4)).reshape(k // 512, 4)
    idx = np.arange(k)
    return np.exp2(a[idx // 512, idx % 128 // 32])


BF16 = ml_dtypes.bfloat16


def bf(x):
    return np.asarray(x, np.float32).astype(BF16)


def f64(x):
    return np.asarray(x).astype(np.float64)


E2M1 = np.array([0.0, 0.5, 1.0, 1.5, 2.0, 3.0, 4.0, 6.0, -0.0, -0.5, -1.0, -1.5, -2.0, -3.0, -4.0, -6.0])


def pack_weight(w, fmt):
    k, n = w.shape
    w = f64(bf(w)).reshape(k // 32, 32, n)
    amax = np.abs(w).max(1)
    if fmt == "e4m3":
        byte = np.frexp(amax)[1] - 1 + 127 - 7
    else:
        mant, ex = np.frexp(amax / 6.0)
        byte = np.where(mant > 0.5, ex, ex - 1) + 127
    byte = np.clip(np.where(amax > 0, byte, 1), 1, 254)
    scaled = (w * np.exp2(127.0 - byte)[:, None, :]).reshape(k, n).astype(np.float32)
    by_word = np.ascontiguousarray(scaled.reshape(k // 512, 128, 4, n).transpose(0, 1, 3, 2))
    if fmt == "e4m3":
        words = by_word.astype(ml_dtypes.float8_e4m3fn).view(np.uint8)
    else:
        c = by_word.astype(ml_dtypes.float4_e2m1fn).view(np.uint8) & 0xF
        words = c[..., 0::2] | (c[..., 1::2] << 4)
    return np.ascontiguousarray(words), np.ascontiguousarray(byte.astype(np.uint8).reshape(k // 512, 16, n))


def unpack_weight(words, scales, fmt):
    g, p, n, _ = words.shape
    if fmt == "e4m3":
        vals = np.ascontiguousarray(words).view(ml_dtypes.float8_e4m3fn).astype(np.float64)
    else:
        nib = np.empty((g, p, n, 4), np.uint8)
        nib[..., 0::2] = words & 0xF
        nib[..., 1::2] = words >> 4
        vals = E2M1[nib]
    vals = vals * np.repeat(np.exp2(scales.astype(np.float64) - 127.0), 8, axis=1)[..., None]
    return vals.transpose(0, 1, 3, 2).reshape(g * 512, n)


T, B, D_IN, D_H, D_K, D_OUT = 2, 4096, 512, 1024, 512, 256


def setup_inputs():
    s, t = mx_kscale(D_H), mx_kscale(D_K)
    h1 = bf(np.maximum(np.random.standard_normal((T, B, D_H)), 0.0) * s)
    W2 = np.random.standard_normal((T, D_H, D_K)) * 1.4 / np.sqrt(D_H) / s[:, None] * t
    W2_words, W2_scales = pack_weight(W2.reshape(-1, D_K), "e4m3")
    b2 = bf(np.random.standard_normal((T, D_K)) * 0.2 * t)
    W3 = np.random.standard_normal((T, D_K, D_OUT)) * 1.4 / np.sqrt(D_K) / t[:, None]
    W3_words, W3_scales = pack_weight(W3.reshape(-1, D_OUT), "e4m3")
    b3 = bf(np.random.standard_normal((T, D_OUT)) * 0.2)
    return {"h1": h1,
            "W2_words": W2_words,
            "W2_scales": W2_scales,
            "b2": b2,
            "W3_words": W3_words,
            "W3_scales": W3_scales,
            "b3": b3}


def reference(h1, W2_words, W2_scales, b2, W3_words, W3_scales, b3):
    h2 = np.maximum((mxq(f64(h1), 2, "e4m3") @ unpack_weight(W2_words, W2_scales, "e4m3").reshape(T, D_H, D_K)) + f64(b2)[:, None, :], 0.0)
    out = (mxq(h2, 2, "e4m3") @ unpack_weight(W3_words, W3_scales, "e4m3").reshape(T, D_K, D_OUT)) + f64(b3)[:, None, :]
    return out.mean(axis=0)

@@ -1,0 +1,255 @@
+from contextlib import ExitStack
+
+import concourse.mybir as mybir
+from concourse.masks import make_identity
+
+F32 = mybir.dt.float32
+BF16 = mybir.dt.bfloat16
+I32 = mybir.dt.int32
+U32 = mybir.dt.uint32
+U8 = mybir.dt.uint8
+FP8X4 = mybir.dt.float8_e4m3fn_x4
+ADD = mybir.AluOpType.add
+MULT = mybir.AluOpType.mult
+RELU = mybir.ActivationFunctionType.Relu
+
+TREES, BATCH, D_H, D_K, D_OUT = 2, 4096, 1024, 512, 256
+P = 128
+PACK = 4
+K_PASS = P * PACK
+PASSES1 = D_H // K_PASS
+PLANES = 2
+WORDS_PASS = K_PASS // 2
+ROUNDS = BATCH // P
+LOAD_ROUNDS = 2
+STORE_ROUNDS = 2
+QUADRANTS = 4
+SCALE_ROWS = 4
+
+FLOPS = 2 * TREES * BATCH * (D_H * D_K + D_K * D_OUT)
+
+
+def tile_randomforestmlp_pa_t_e_kernel(
+    tc, h1, W2_words, W2_scales, b2, W3_words, W3_scales, b3, out
+):
+    nc = tc.nc
+    h1_rows = [h1[e].rearrange("(p r) k -> p r k", r=ROUNDS) for e in range(TREES)]
+    out_rows = out.rearrange("(p r) n -> p r n", r=ROUNDS)
+
+    with ExitStack() as ctx:
+        ctx.enter_context(tc.manual_schedule())
+        consts = ctx.enter_context(tc.tile_pool(name="consts", bufs=1))
+        resident = ctx.enter_context(tc.tile_pool(name="resident", bufs=1))
+        work = ctx.enter_context(tc.tile_pool(name="work", bufs=2))
+        psum_h1t = ctx.enter_context(tc.psum_pool(name="psum_h1t", bufs=4))
+        psum_acc1 = ctx.enter_context(tc.psum_pool(name="psum_acc1", bufs=2))
+        psum_h2t = ctx.enter_context(tc.psum_pool(name="psum_h2t", bufs=1))
+        psum_acc2 = ctx.enter_context(tc.psum_pool(name="psum_acc2", bufs=1))
+
+        ident = consts.tile([P, P], F32, name="ident")
+        make_identity(nc, ident[:])
+
+        w2_planes = consts.tile([P, D_K], U8, name="w2_planes", align_bytes=64)
+        w3_planes = consts.tile([P, D_OUT], U8, name="w3_planes", align_bytes=64)
+        nc.vector.memset(w2_planes[:].bitcast(I32), 0)
+        nc.vector.memset(w3_planes[:].bitcast(I32), 0)
+        w2 = consts.tile([P, TREES * PASSES1, D_K], U32, name="w2", align_bytes=64)
+        w3 = consts.tile([P, TREES, D_OUT], U32, name="w3", align_bytes=64)
+
+        ones = consts.tile([P, P], BF16, name="ones")
+        b2_rows = consts.tile([P, TREES * D_K], BF16, name="b2_rows")
+        b3_rows = consts.tile([P, D_OUT], BF16, name="b3_rows")
+        nc.vector.memset(ones[:], 1.0)
+        nc.vector.memset(b2_rows[:], 0.0)
+        nc.vector.memset(b3_rows[:], 0.0)
+        nc.scalar.dma_start(out=b2_rows[0:1, :], in_=b2.rearrange("e k -> (e k)").unsqueeze(0))
+        nc.scalar.dma_start(out=b3_rows[0:TREES, :], in_=b3)
+
+        h1_sb = {}
+
+        def load_h1(c):
+            for e in range(TREES):
+                x = resident.tile([P, LOAD_ROUNDS, D_H], BF16, name="h1_t%d_c%d" % (e, c))
+                rounds = slice(c * LOAD_ROUNDS, (c + 1) * LOAD_ROUNDS)
+                nc.sync.dma_start(out=x[:], in_=h1_rows[e][:, rounds, :])
+                h1_sb[(e, c)] = x
+
+        def load_weight(words_sb, planes_sb, words, scales):
+            passes = words.shape[0]
+            for q in range(QUADRANTS):
+                nc.sync.dma_start(
+                    out=planes_sb[32 * q : 32 * q + SCALE_ROWS * passes, :].bitcast(I32),
+                    in_=scales[:, SCALE_ROWS * q : SCALE_ROWS * (q + 1), :].bitcast(I32),
+                )
+            for g in range(passes):
+                nc.sync.dma_start(
+                    out=words_sb[:, g, :].bitcast(I32),
+                    in_=words[g].rearrange("p n t -> p (n t)").bitcast(I32),
+                )
+
+        load_h1(0)
+        load_weight(w2, w2_planes, W2_words, W2_scales)
+        load_h1(1)
+        load_weight(w3, w3_planes, W3_words, W3_scales)
+        for c in range(2, ROUNDS // LOAD_ROUNDS):
+            load_h1(c)
+
+        b2_wide = consts.tile([P, TREES, D_K], F32, name="b2_wide")
+        for e in range(TREES):
+            spread = psum_acc1.tile([P, D_K], F32, name="acc1")
+            nc.tensor.matmul(
+                out=spread[:], lhsT=ones[:], rhs=b2_rows[:, e * D_K : (e + 1) * D_K],
+                start=True, stop=True,
+            )
+            nc.vector.tensor_copy(
+                out=b2_wide[:, e, :].rearrange("p (u q c) -> p u q c", u=PLANES, c=2),
+                in_=spread[:].rearrange("p (q u c) -> p u q c", u=PLANES, c=2),
+            )
+        b3_half = consts.tile([P, D_OUT], F32, name="b3_half")
+        spread3 = psum_acc2.tile([P, D_OUT], F32, name="acc2")
+        nc.tensor.matmul(out=spread3[:], lhsT=ones[:], rhs=b3_rows[:], start=True, stop=True)
+        nc.vector.tensor_scalar_mul(out=b3_half[:], in0=spread3[:], scalar1=1.0 / TREES)
+
+        h1t, h1_grouped, h1_q = {}, {}, {}
+        acc1, h2_rows, h2t, h2_grouped, h2_q = {}, {}, {}, {}, {}
+        acc2, out_sb = {}, {}
+
+        def transpose_h1(r):
+            c, j = divmod(r, LOAD_ROUNDS)
+            for e in range(TREES):
+                words = h1_sb[(e, c)][:].bitcast(F32)
+                bank = psum_h1t.tile([P, PASSES1, PLANES, P], F32, name="h1t")
+                for g in range(PASSES1):
+                    for u in range(PLANES):
+                        nc.tensor.transpose(
+                            bank[:, g, u, :],
+                            words[:, j, WORDS_PASS * g + u : WORDS_PASS * (g + 1) : PLANES],
+                            ident[:],
+                        )
+                h1t[(r, e)] = bank
+
+        def regroup_h1(r):
+            grouped = work.tile(
+                [P, TREES, PASSES1, P, PACK], BF16, name="h1_grouped", align_bytes=64
+            )
+            for e in range(TREES):
+                nc.scalar.copy(
+                    out=grouped[:, e].bitcast(F32),
+                    in_=h1t[(r, e)][:].rearrange("p g u b -> p g b u"),
+                )
+            h1_grouped[r] = grouped
+
+        def quantise_h1(r):
+            codes = work.tile([P, TREES * PASSES1 * P], U32, name="h1_codes", align_bytes=64)
+            scales = work.tile([P, TREES * PASSES1 * P], U8, name="h1_scales", align_bytes=64)
+            nc.vector.quantize_mx(
+                out=codes[:].bitcast(FP8X4),
+                scales=scales[:],
+                in_=h1_grouped[r][:].rearrange("p e g b t -> p (e g b t)"),
+            )
+            h1_q[r] = (codes, scales)
+
+        def first_layer(r):
+            codes, scales = h1_q[r]
+            for e in range(TREES):
+                sums = psum_acc1.tile([P, D_K], F32, name="acc1")
+                for g in range(PASSES1):
+                    w = e * PASSES1 + g
+                    cols = slice(w * P, (w + 1) * P)
+                    nc.tensor.matmul_mx(
+                        out=sums[:],
+                        lhsT=codes[:, cols].bitcast(FP8X4),
+                        lhsT_scale=scales[:, cols],
+                        rhs=w2[:, w, :].bitcast(FP8X4),
+                        rhs_scale=w2_planes[SCALE_ROWS * w : P, :],
+                        start=(g == 0),
+                        stop=(g == PASSES1 - 1),
+                    )
+                acc1[(r, e)] = sums
+
+        def add_bias(r):
+            rows = work.tile([P, TREES, D_K], BF16, name="h2_rows")
+            for e in range(TREES):
+                nc.vector.tensor_tensor(
+                    out=rows[:, e, :].rearrange("p (u q c) -> p u q c", u=PLANES, c=2),
+                    in0=acc1[(r, e)][:].rearrange("p (q u c) -> p u q c", u=PLANES, c=2),
+                    in1=b2_wide[:, e, :].rearrange("p (u q c) -> p u q c", u=PLANES, c=2),
+                    op=ADD,
+                )
+            h2_rows[r] = rows
+
+        def transpose_h2(r):
+            words = h2_rows[r][:].bitcast(F32)
+            bank = psum_h2t.tile([P, TREES, PLANES, P], F32, name="h2t")
+            for e in range(TREES):
+                for u in range(PLANES):
+                    nc.tensor.transpose(bank[:, e, u, :], words[:, e, u * P : (u + 1) * P], ident[:])
+            h2t[r] = bank
+
+        def relu_regroup_h2(r):
+            grouped = work.tile([P, TREES, P, PACK], BF16, name="h2_grouped", align_bytes=64)
+            for e in range(TREES):
+                nc.scalar.activation(
+                    out=grouped[:, e].rearrange("p b (u c) -> p b u c", c=2),
+                    in_=h2t[r][:, e].bitcast(BF16).rearrange("p u (b c) -> p b u c", c=2),
+                    func=RELU,
+                )
+            h2_grouped[r] = grouped
+
+        def quantise_h2(r):
+            codes = work.tile([P, TREES * P], U32, name="h2_codes", align_bytes=64)
+            scales = work.tile([P, TREES * P], U8, name="h2_scales", align_bytes=64)
+            nc.vector.quantize_mx(
+                out=codes[:].bitcast(FP8X4),
+                scales=scales[:],
+                in_=h2_grouped[r][:].rearrange("p e b t -> p (e b t)"),
+            )
+            h2_q[r] = (codes, scales)
+
+        def second_layer(r):
+            codes, scales = h2_q[r]
+            sums = psum_acc2.tile([P, D_OUT], F32, name="acc2")
+            for e in range(TREES):
+                cols = slice(e * P, (e + 1) * P)
+                nc.tensor.matmul_mx(
+                    out=sums[:],
+                    lhsT=codes[:, cols].bitcast(FP8X4),
+                    lhsT_scale=scales[:, cols],
+                    rhs=w3[:, e, :].bitcast(FP8X4),
+                    rhs_scale=w3_planes[SCALE_ROWS * e : P, :],
+                    start=(e == 0),
+                    stop=(e == TREES - 1),
+                )
+            acc2[r] = sums
+
+        def finish(r):
+            c, j = divmod(r, STORE_ROUNDS)
+            if j == 0:
+                out_sb[c] = resident.tile([P, STORE_ROUNDS, D_OUT], F32, name="out_c%d" % c)
+            nc.vector.scalar_tensor_tensor(
+                out=out_sb[c][:, j, :], in0=acc2[r][:], scalar=1.0 / TREES, in1=b3_half[:],
+                op0=MULT, op1=ADD,
+            )
+            if j == STORE_ROUNDS - 1:
+                rounds = slice(c * STORE_ROUNDS, (c + 1) * STORE_ROUNDS)
+                nc.sync.dma_start(out=out_rows[:, rounds, :], in_=out_sb[c][:])
+
+        def live(r):
+            return 0 <= r < ROUNDS
+
+        for i in range(ROUNDS + 3):
+            if live(i):
+                transpose_h1(i)
+                regroup_h1(i)
+                quantise_h1(i)
+            if live(i - 2):
+                transpose_h2(i - 2)
+                relu_regroup_h2(i - 2)
+            if live(i - 1):
+                first_layer(i - 1)
+                add_bias(i - 1)
+            if live(i - 2):
+                quantise_h2(i - 2)
+            if live(i - 3):
+                second_layer(i - 3)
+                finish(i - 3)

@@ -168,7 +168,7 @@ def tile_randomforestmlp_pa_t_e_kernel(
                 acc1[(r, e)] = sums
 
         def add_bias(r):
-            rows = work.tile([P, TREES, D_K], BF16, name="h2_rows")
+            rows = work.tile([P, TREES, D_K], BF16, name="h2_rows", bufs=3)
             for e in range(TREES):
                 nc.vector.tensor_tensor(
                     out=rows[:, e, :].rearrange("p (u q c) -> p u q c", u=PLANES, c=2),
@@ -237,19 +237,19 @@ def tile_randomforestmlp_pa_t_e_kernel(
         def live(r):
             return 0 <= r < ROUNDS
 
-        for i in range(ROUNDS + 3):
+        for i in range(ROUNDS + 4):
             if live(i):
                 transpose_h1(i)
                 regroup_h1(i)
                 quantise_h1(i)
-            if live(i - 2):
-                transpose_h2(i - 2)
-                relu_regroup_h2(i - 2)
+            if live(i - 3):
+                transpose_h2(i - 3)
+                relu_regroup_h2(i - 3)
             if live(i - 1):
                 first_layer(i - 1)
                 add_bias(i - 1)
-            if live(i - 2):
-                quantise_h2(i - 2)
             if live(i - 3):
-                second_layer(i - 3)
-                finish(i - 3)
+                quantise_h2(i - 3)
+            if live(i - 4):
+                second_layer(i - 4)
+                finish(i - 4)

@@ -21,7 +21,6 @@ PASSES1 = D_H // K_PASS
 PLANES = 2
 WORDS_PASS = K_PASS // 2
 ROUNDS = BATCH // P
-LOAD_ROUNDS = 2
 STORE_ROUNDS = 2
 QUADRANTS = 4
 SCALE_ROWS = 4
@@ -41,8 +40,8 @@ def tile_randomforestmlp_pa_t_e_kernel(
         consts = ctx.enter_context(tc.tile_pool(name="consts", bufs=1))
         resident = ctx.enter_context(tc.tile_pool(name="resident", bufs=1))
         work = ctx.enter_context(tc.tile_pool(name="work", bufs=2))
-        psum_h1t = ctx.enter_context(tc.psum_pool(name="psum_h1t", bufs=4))
-        psum_acc1 = ctx.enter_context(tc.psum_pool(name="psum_acc1", bufs=2))
+        psum_h1t = ctx.enter_context(tc.psum_pool(name="psum_h1t", bufs=3))
+        psum_acc1 = ctx.enter_context(tc.psum_pool(name="psum_acc1", bufs=3))
         psum_h2t = ctx.enter_context(tc.psum_pool(name="psum_h2t", bufs=1))
         psum_acc2 = ctx.enter_context(tc.psum_pool(name="psum_acc2", bufs=1))
 
@@ -67,12 +66,11 @@ def tile_randomforestmlp_pa_t_e_kernel(
 
         h1_sb = {}
 
-        def load_h1(c):
+        def load_h1(r):
             for e in range(TREES):
-                x = resident.tile([P, LOAD_ROUNDS, D_H], BF16, name="h1_t%d_c%d" % (e, c))
-                rounds = slice(c * LOAD_ROUNDS, (c + 1) * LOAD_ROUNDS)
-                nc.sync.dma_start(out=x[:], in_=h1_rows[e][:, rounds, :])
-                h1_sb[(e, c)] = x
+                x = resident.tile([P, D_H], BF16, name="h1_r%d_t%d" % (r, e))
+                nc.sync.dma_start(out=x[:], in_=h1_rows[e][:, r, :])
+                h1_sb[(r, e)] = x
 
         def load_weight(words_sb, planes_sb, words, scales):
             passes = words.shape[0]
@@ -88,11 +86,13 @@ def tile_randomforestmlp_pa_t_e_kernel(
                 )
 
         load_h1(0)
-        load_weight(w2, w2_planes, W2_words, W2_scales)
         load_h1(1)
+        load_weight(w2, w2_planes, W2_words, W2_scales)
+        load_h1(2)
+        load_h1(3)
         load_weight(w3, w3_planes, W3_words, W3_scales)
-        for c in range(2, ROUNDS // LOAD_ROUNDS):
-            load_h1(c)
+        for r in range(4, ROUNDS):
+            load_h1(r)
 
         b2_wide = consts.tile([P, TREES, D_K], F32, name="b2_wide")
         for e in range(TREES):
@@ -115,15 +115,14 @@ def tile_randomforestmlp_pa_t_e_kernel(
         acc2, out_sb = {}, {}
 
         def transpose_h1(r):
-            c, j = divmod(r, LOAD_ROUNDS)
             for e in range(TREES):
-                words = h1_sb[(e, c)][:].bitcast(F32)
+                words = h1_sb[(r, e)][:].bitcast(F32)
                 bank = psum_h1t.tile([P, PASSES1, PLANES, P], F32, name="h1t")
                 for g in range(PASSES1):
                     for u in range(PLANES):
                         nc.tensor.transpose(
                             bank[:, g, u, :],
-                            words[:, j, WORDS_PASS * g + u : WORDS_PASS * (g + 1) : PLANES],
+                            words[:, WORDS_PASS * g + u : WORDS_PASS * (g + 1) : PLANES],
                             ident[:],
                         )
                 h1t[(r, e)] = bank

@@ -21,8 +21,7 @@ PASSES1 = D_H // K_PASS
 PLANES = 2
 WORDS_PASS = K_PASS // 2
 ROUNDS = BATCH // P
-STORE_ROUNDS = 2
-QUADRANTS = 4
+QUADRANT = 32
 SCALE_ROWS = 4
 
 FLOPS = 2 * TREES * BATCH * (D_H * D_K + D_K * D_OUT)
@@ -63,6 +62,8 @@ def tile_randomforestmlp_pa_t_e_kernel(
         nc.vector.memset(b3_rows[:], 0.0)
         nc.scalar.dma_start(out=b2_rows[0:1, :], in_=b2.rearrange("e k -> (e k)").unsqueeze(0))
         nc.scalar.dma_start(out=b3_rows[0:TREES, :], in_=b3)
+        b2_wide = consts.tile([P, TREES, D_K], F32, name="b2_wide")
+        b3_half = consts.tile([P, D_OUT], F32, name="b3_half")
 
         h1_sb = {}
 
@@ -74,9 +75,10 @@ def tile_randomforestmlp_pa_t_e_kernel(
 
         def load_weight(words_sb, planes_sb, words, scales):
             passes = words.shape[0]
-            for q in range(QUADRANTS):
+            for q in range(P // QUADRANT):
+                first = QUADRANT * q
                 nc.sync.dma_start(
-                    out=planes_sb[32 * q : 32 * q + SCALE_ROWS * passes, :].bitcast(I32),
+                    out=planes_sb[first : first + SCALE_ROWS * passes, :].bitcast(I32),
                     in_=scales[:, SCALE_ROWS * q : SCALE_ROWS * (q + 1), :].bitcast(I32),
                 )
             for g in range(passes):
@@ -94,25 +96,24 @@ def tile_randomforestmlp_pa_t_e_kernel(
         for r in range(4, ROUNDS):
             load_h1(r)
 
-        b2_wide = consts.tile([P, TREES, D_K], F32, name="b2_wide")
-        for e in range(TREES):
-            spread = psum_acc1.tile([P, D_K], F32, name="acc1")
-            nc.tensor.matmul(
-                out=spread[:], lhsT=ones[:], rhs=b2_rows[:, e * D_K : (e + 1) * D_K],
-                start=True, stop=True,
-            )
-            nc.vector.tensor_copy(
-                out=b2_wide[:, e, :].rearrange("p (u q c) -> p u q c", u=PLANES, c=2),
-                in_=spread[:].rearrange("p (q u c) -> p u q c", u=PLANES, c=2),
-            )
-        b3_half = consts.tile([P, D_OUT], F32, name="b3_half")
-        spread3 = psum_acc2.tile([P, D_OUT], F32, name="acc2")
-        nc.tensor.matmul(out=spread3[:], lhsT=ones[:], rhs=b3_rows[:], start=True, stop=True)
-        nc.vector.tensor_scalar_mul(out=b3_half[:], in0=spread3[:], scalar1=1.0 / TREES)
+        def spread_biases():
+            for e in range(TREES):
+                spread = psum_acc1.tile([P, D_K], F32, name="acc1")
+                nc.tensor.matmul(
+                    out=spread[:], lhsT=ones[:], rhs=b2_rows[:, e * D_K : (e + 1) * D_K],
+                    start=True, stop=True,
+                )
+                nc.vector.tensor_copy(
+                    out=b2_wide[:, e, :].rearrange("p (u q h) -> p u q h", u=PLANES, h=2),
+                    in_=spread[:].rearrange("p (q u h) -> p u q h", u=PLANES, h=2),
+                )
+            spread = psum_acc2.tile([P, D_OUT], F32, name="acc2")
+            nc.tensor.matmul(out=spread[:], lhsT=ones[:], rhs=b3_rows[:], start=True, stop=True)
+            nc.vector.tensor_scalar_mul(out=b3_half[:], in0=spread[:], scalar1=1.0 / TREES)
 
         h1t, h1_grouped, h1_q = {}, {}, {}
         acc1, h2_rows, h2t, h2_grouped, h2_q = {}, {}, {}, {}, {}
-        acc2, out_sb = {}, {}
+        acc2 = {}
 
         def transpose_h1(r):
             for e in range(TREES):
@@ -170,9 +171,9 @@ def tile_randomforestmlp_pa_t_e_kernel(
             rows = work.tile([P, TREES, D_K], BF16, name="h2_rows", bufs=3)
             for e in range(TREES):
                 nc.vector.tensor_tensor(
-                    out=rows[:, e, :].rearrange("p (u q c) -> p u q c", u=PLANES, c=2),
-                    in0=acc1[(r, e)][:].rearrange("p (q u c) -> p u q c", u=PLANES, c=2),
-                    in1=b2_wide[:, e, :].rearrange("p (u q c) -> p u q c", u=PLANES, c=2),
+                    out=rows[:, e, :].rearrange("p (u q h) -> p u q h", u=PLANES, h=2),
+                    in0=acc1[(r, e)][:].rearrange("p (q u h) -> p u q h", u=PLANES, h=2),
+                    in1=b2_wide[:, e, :].rearrange("p (u q h) -> p u q h", u=PLANES, h=2),
                     op=ADD,
                 )
             h2_rows[r] = rows
@@ -189,8 +190,8 @@ def tile_randomforestmlp_pa_t_e_kernel(
             grouped = work.tile([P, TREES, P, PACK], BF16, name="h2_grouped", align_bytes=64)
             for e in range(TREES):
                 nc.scalar.activation(
-                    out=grouped[:, e].rearrange("p b (u c) -> p b u c", c=2),
-                    in_=h2t[r][:, e].bitcast(BF16).rearrange("p u (b c) -> p b u c", c=2),
+                    out=grouped[:, e].rearrange("p b (u h) -> p b u h", h=2),
+                    in_=h2t[r][:, e].bitcast(BF16).rearrange("p u (b h) -> p b u h", h=2),
                     func=RELU,
                 )
             h2_grouped[r] = grouped
@@ -222,21 +223,17 @@ def tile_randomforestmlp_pa_t_e_kernel(
             acc2[r] = sums
 
         def finish(r):
-            c, j = divmod(r, STORE_ROUNDS)
-            if j == 0:
-                out_sb[c] = resident.tile([P, STORE_ROUNDS, D_OUT], F32, name="out_c%d" % c)
+            result = resident.tile([P, D_OUT], F32, name="out_r%d" % r)
             nc.vector.scalar_tensor_tensor(
-                out=out_sb[c][:, j, :], in0=acc2[r][:], scalar=1.0 / TREES, in1=b3_half[:],
+                out=result[:], in0=acc2[r][:], scalar=1.0 / TREES, in1=b3_half[:],
                 op0=MULT, op1=ADD,
             )
-            if j == STORE_ROUNDS - 1:
-                rounds = slice(c * STORE_ROUNDS, (c + 1) * STORE_ROUNDS)
-                nc.sync.dma_start(out=out_rows[:, rounds, :], in_=out_sb[c][:])
+            nc.sync.dma_start(out=out_rows[:, r, :], in_=result[:])
 
         def live(r):
             return 0 <= r < ROUNDS
 
-        for i in range(ROUNDS + 4):
+        def step(i):
             if live(i):
                 transpose_h1(i)
                 regroup_h1(i)
@@ -252,3 +249,8 @@ def tile_randomforestmlp_pa_t_e_kernel(
             if live(i - 4):
                 second_layer(i - 4)
                 finish(i - 4)
+
+        step(0)
+        spread_biases()
+        for i in range(1, ROUNDS + 4):
+            step(i)

@@ -21,8 +21,14 @@ PASSES1 = D_H // K_PASS
 PLANES = 2
 WORDS_PASS = K_PASS // 2
 ROUNDS = BATCH // P
+CHUNK = 4
+UNIT_ROWS = CHUNK * P
+CHUNKS = ROUNDS // CHUNK
+UNITS = CHUNKS * TREES
+HALF = CHUNK // 2
 QUADRANT = 32
 SCALE_ROWS = 4
+AHEAD = 6
 
 FLOPS = 2 * TREES * BATCH * (D_H * D_K + D_K * D_OUT)
 
@@ -37,87 +43,110 @@ def tile_randomforestmlp_pa_t_e_kernel(
     with ExitStack() as ctx:
         ctx.enter_context(tc.manual_schedule())
         consts = ctx.enter_context(tc.tile_pool(name="consts", bufs=1))
-        resident = ctx.enter_context(tc.tile_pool(name="resident", bufs=1))
+        h1_pool = ctx.enter_context(tc.tile_pool(name="h1_pool", bufs=(AHEAD + 1) * CHUNK))
         work = ctx.enter_context(tc.tile_pool(name="work", bufs=2))
         psum_h1t = ctx.enter_context(tc.psum_pool(name="psum_h1t", bufs=3))
-        psum_acc1 = ctx.enter_context(tc.psum_pool(name="psum_acc1", bufs=3))
-        psum_h2t = ctx.enter_context(tc.psum_pool(name="psum_h2t", bufs=1))
+        psum_acc1 = ctx.enter_context(tc.psum_pool(name="psum_acc1", bufs=4))
         psum_acc2 = ctx.enter_context(tc.psum_pool(name="psum_acc2", bufs=1))
 
         ident = consts.tile([P, P], F32, name="ident")
         make_identity(nc, ident[:])
 
+        warm = consts.tile([P, 2], F32, name="warm")
+        nc.vector.memset(warm[:], 0.0)
+        nc.scalar.activation(out=warm[:, 1:2], in_=warm[:, 0:1], func=RELU)
+
+        w2_planes_raw = consts.tile([P, D_K], U8, name="w2_planes_raw", align_bytes=64)
         w2_planes = consts.tile([P, D_K], U8, name="w2_planes", align_bytes=64)
         w3_planes = consts.tile([P, D_OUT], U8, name="w3_planes", align_bytes=64)
-        nc.vector.memset(w2_planes[:].bitcast(I32), 0)
+        nc.vector.memset(w2_planes_raw[:].bitcast(I32), 0)
         nc.vector.memset(w3_planes[:].bitcast(I32), 0)
+        w2_raw = consts.tile([P, TREES * PASSES1, D_K], U32, name="w2_raw", align_bytes=64)
         w2 = consts.tile([P, TREES * PASSES1, D_K], U32, name="w2", align_bytes=64)
         w3 = consts.tile([P, TREES, D_OUT], U32, name="w3", align_bytes=64)
 
+        b2_cols_bf = consts.tile([P, TREES, PACK], BF16, name="b2_cols_bf")
+        b2_cols = consts.tile([P, TREES, PACK], F32, name="b2_cols")
+        nc.scalar.dma_start(out=b2_cols_bf[:], in_=b2.rearrange("e (p t) -> p e t", t=PACK))
+
         ones = consts.tile([P, P], BF16, name="ones")
-        b2_rows = consts.tile([P, TREES * D_K], BF16, name="b2_rows")
-        b3_rows = consts.tile([P, D_OUT], BF16, name="b3_rows")
+        b3_rows = consts.tile([P, HALF, D_OUT], BF16, name="b3_rows")
         nc.vector.memset(ones[:], 1.0)
-        nc.vector.memset(b2_rows[:], 0.0)
         nc.vector.memset(b3_rows[:], 0.0)
-        nc.scalar.dma_start(out=b2_rows[0:1, :], in_=b2.rearrange("e k -> (e k)").unsqueeze(0))
-        nc.scalar.dma_start(out=b3_rows[0:TREES, :], in_=b3)
-        b2_wide = consts.tile([P, TREES, D_K], F32, name="b2_wide")
-        b3_half = consts.tile([P, D_OUT], F32, name="b3_half")
+        for j in range(HALF):
+            nc.scalar.dma_start(out=b3_rows[0:TREES, j, :], in_=b3)
+        b3_half = consts.tile([P, HALF, D_OUT], F32, name="b3_half")
+        nc.vector.tensor_copy(out=b2_cols[:], in_=b2_cols_bf[:])
 
         h1_sb = {}
 
-        def load_h1(r):
-            for e in range(TREES):
-                x = resident.tile([P, D_H], BF16, name="h1_r%d_t%d" % (r, e))
-                nc.sync.dma_start(out=x[:], in_=h1_rows[e][:, r, :])
-                h1_sb[(r, e)] = x
+        def load_h1(n):
+            c, e = divmod(n, TREES)
+            for i in range(CHUNK):
+                x = h1_pool.tile([P, D_H], BF16, name="h1_sb")
+                nc.sync.dma_start(out=x[:], in_=h1_rows[e][:, CHUNK * c + i, :])
+                h1_sb[(n, i)] = x
 
-        def load_weight(words_sb, planes_sb, words, scales):
-            passes = words.shape[0]
+        def load_planes(planes_sb, scales):
+            passes = scales.shape[0]
             for q in range(P // QUADRANT):
                 first = QUADRANT * q
                 nc.sync.dma_start(
                     out=planes_sb[first : first + SCALE_ROWS * passes, :].bitcast(I32),
                     in_=scales[:, SCALE_ROWS * q : SCALE_ROWS * (q + 1), :].bitcast(I32),
                 )
-            for g in range(passes):
-                nc.sync.dma_start(
-                    out=words_sb[:, g, :].bitcast(I32),
-                    in_=words[g].rearrange("p n t -> p (n t)").bitcast(I32),
-                )
+
+        def load_words(words_sb, words, g):
+            nc.sync.dma_start(
+                out=words_sb[:, g, :].bitcast(I32),
+                in_=words[g].rearrange("p n t -> p (n t)").bitcast(I32),
+            )
 
         load_h1(0)
+        load_planes(w2_planes_raw, W2_scales)
+        load_words(w2_raw, W2_words, 0)
+        load_words(w2_raw, W2_words, 1)
         load_h1(1)
-        load_weight(w2, w2_planes, W2_words, W2_scales)
-        load_h1(2)
-        load_h1(3)
-        load_weight(w3, w3_planes, W3_words, W3_scales)
-        for r in range(4, ROUNDS):
-            load_h1(r)
+        load_words(w2_raw, W2_words, 2)
+        load_words(w2_raw, W2_words, 3)
+        load_planes(w3_planes, W3_scales)
+        load_words(w3, W3_words, 0)
+        load_words(w3, W3_words, 1)
+        for n in range(2, AHEAD):
+            load_h1(n)
 
-        def spread_biases():
-            for e in range(TREES):
-                spread = psum_acc1.tile([P, D_K], F32, name="acc1")
-                nc.tensor.matmul(
-                    out=spread[:], lhsT=ones[:], rhs=b2_rows[:, e * D_K : (e + 1) * D_K],
-                    start=True, stop=True,
-                )
-                nc.vector.tensor_copy(
-                    out=b2_wide[:, e, :].rearrange("p (u q h) -> p u q h", u=PLANES, h=2),
-                    in_=spread[:].rearrange("p (q u h) -> p u q h", u=PLANES, h=2),
-                )
-            spread = psum_acc2.tile([P, D_OUT], F32, name="acc2")
-            nc.tensor.matmul(out=spread[:], lhsT=ones[:], rhs=b3_rows[:], start=True, stop=True)
+        def reorder_w2_planes():
+            nc.vector.tensor_copy(
+                out=w2_planes[:].rearrange("p (t m) -> p m t", t=PACK),
+                in_=w2_planes_raw[:].rearrange("p (m t) -> p m t", t=PACK),
+            )
+
+        def reorder_w2(w):
+            nc.vector.tensor_copy(
+                out=w2[:, w, :].bitcast(I32).rearrange("p (t m) -> p t m", t=PACK),
+                in_=w2_raw[:, w, :].bitcast(I32).rearrange("p (m t) -> p t m", t=PACK),
+            )
+
+        def spread_b3():
+            spread = psum_acc2.tile([P, HALF, D_OUT], F32, name="acc2")
+            nc.tensor.matmul(
+                out=spread[:].rearrange("p j n -> p (j n)"),
+                lhsT=ones[:],
+                rhs=b3_rows[:].rearrange("p j n -> p (j n)"),
+                start=True, stop=True,
+            )
             nc.vector.tensor_scalar_mul(out=b3_half[:], in0=spread[:], scalar1=1.0 / TREES)
 
-        h1t, h1_grouped, h1_q = {}, {}, {}
-        acc1, h2_rows, h2t, h2_grouped, h2_q = {}, {}, {}, {}, {}
-        acc2 = {}
+        h1_grouped, h1_q = {}, {}
+        h2_slots, h2_grouped, h2_q = {}, {}, {}
+        acc2, result = {}, {}
 
-        def transpose_h1(r):
-            for e in range(TREES):
-                words = h1_sb[(r, e)][:].bitcast(F32)
+        def transpose_h1(n):
+            grouped = work.tile(
+                [P, PASSES1, CHUNK, P, PACK], BF16, name="h1_grouped", align_bytes=64
+            )
+            for i in range(CHUNK):
+                words = h1_sb[(n, i)][:].bitcast(F32)
                 bank = psum_h1t.tile([P, PASSES1, PLANES, P], F32, name="h1t")
                 for g in range(PASSES1):
                     for u in range(PLANES):
@@ -126,131 +155,118 @@ def tile_randomforestmlp_pa_t_e_kernel(
                             words[:, WORDS_PASS * g + u : WORDS_PASS * (g + 1) : PLANES],
                             ident[:],
                         )
-                h1t[(r, e)] = bank
+                dst = grouped[:, :, i].bitcast(F32)
+                src = bank[:].rearrange("p g u b -> p g b u")
+                if i < CHUNK - 1:
+                    nc.scalar.copy(out=dst, in_=src)
+                else:
+                    nc.vector.tensor_copy(out=dst, in_=src)
+            h1_grouped[n] = grouped
 
-        def regroup_h1(r):
-            grouped = work.tile(
-                [P, TREES, PASSES1, P, PACK], BF16, name="h1_grouped", align_bytes=64
-            )
-            for e in range(TREES):
-                nc.scalar.copy(
-                    out=grouped[:, e].bitcast(F32),
-                    in_=h1t[(r, e)][:].rearrange("p g u b -> p g b u"),
-                )
-            h1_grouped[r] = grouped
-
-        def quantise_h1(r):
-            codes = work.tile([P, TREES * PASSES1 * P], U32, name="h1_codes", align_bytes=64)
-            scales = work.tile([P, TREES * PASSES1 * P], U8, name="h1_scales", align_bytes=64)
+        def quantise_h1(n):
+            codes = work.tile([P, PASSES1 * UNIT_ROWS], U32, name="h1_codes", align_bytes=64)
+            scales = work.tile([P, PASSES1 * UNIT_ROWS], U8, name="h1_scales", align_bytes=64)
             nc.vector.quantize_mx(
                 out=codes[:].bitcast(FP8X4),
                 scales=scales[:],
-                in_=h1_grouped[r][:].rearrange("p e g b t -> p (e g b t)"),
+                in_=h1_grouped[n][:].rearrange("p g i b t -> p (g i b t)"),
             )
-            h1_q[r] = (codes, scales)
+            h1_q[n] = (codes, scales)
 
-        def first_layer(r):
-            codes, scales = h1_q[r]
-            for e in range(TREES):
-                sums = psum_acc1.tile([P, D_K], F32, name="acc1")
+        def first_layer(n):
+            e = n % TREES
+            codes, scales = h1_q[n]
+            slots = work.tile([P, PACK, UNIT_ROWS], BF16, name="h2_slots")
+            for t in range(PACK):
+                sums = psum_acc1.tile([P, UNIT_ROWS], F32, name="acc1")
+                chans = slice(t * P, (t + 1) * P)
                 for g in range(PASSES1):
                     w = e * PASSES1 + g
-                    cols = slice(w * P, (w + 1) * P)
+                    cols = slice(g * UNIT_ROWS, (g + 1) * UNIT_ROWS)
                     nc.tensor.matmul_mx(
                         out=sums[:],
-                        lhsT=codes[:, cols].bitcast(FP8X4),
-                        lhsT_scale=scales[:, cols],
-                        rhs=w2[:, w, :].bitcast(FP8X4),
-                        rhs_scale=w2_planes[SCALE_ROWS * w : P, :],
+                        lhsT=w2[:, w, chans].bitcast(FP8X4),
+                        lhsT_scale=w2_planes[SCALE_ROWS * w : P, chans],
+                        rhs=codes[:, cols].bitcast(FP8X4),
+                        rhs_scale=scales[:, cols],
                         start=(g == 0),
                         stop=(g == PASSES1 - 1),
                     )
-                acc1[(r, e)] = sums
-
-        def add_bias(r):
-            rows = work.tile([P, TREES, D_K], BF16, name="h2_rows", bufs=3)
-            for e in range(TREES):
-                nc.vector.tensor_tensor(
-                    out=rows[:, e, :].rearrange("p (u q h) -> p u q h", u=PLANES, h=2),
-                    in0=acc1[(r, e)][:].rearrange("p (q u h) -> p u q h", u=PLANES, h=2),
-                    in1=b2_wide[:, e, :].rearrange("p (u q h) -> p u q h", u=PLANES, h=2),
-                    op=ADD,
-                )
-            h2_rows[r] = rows
-
-        def transpose_h2(r):
-            words = h2_rows[r][:].bitcast(F32)
-            bank = psum_h2t.tile([P, TREES, PLANES, P], F32, name="h2t")
-            for e in range(TREES):
-                for u in range(PLANES):
-                    nc.tensor.transpose(bank[:, e, u, :], words[:, e, u * P : (u + 1) * P], ident[:])
-            h2t[r] = bank
-
-        def relu_regroup_h2(r):
-            grouped = work.tile([P, TREES, P, PACK], BF16, name="h2_grouped", align_bytes=64)
-            for e in range(TREES):
                 nc.scalar.activation(
-                    out=grouped[:, e].rearrange("p b (u h) -> p b u h", h=2),
-                    in_=h2t[r][:, e].bitcast(BF16).rearrange("p u (b h) -> p b u h", h=2),
-                    func=RELU,
+                    out=slots[:, t, :], in_=sums[:], func=RELU, bias=b2_cols[:, e, t : t + 1]
                 )
-            h2_grouped[r] = grouped
+            h2_slots[n] = slots
 
-        def quantise_h2(r):
-            codes = work.tile([P, TREES * P], U32, name="h2_codes", align_bytes=64)
-            scales = work.tile([P, TREES * P], U8, name="h2_scales", align_bytes=64)
+        def regroup_h2(n):
+            grouped = work.tile([P, UNIT_ROWS, PACK], BF16, name="h2_grouped", align_bytes=64)
+            nc.vector.tensor_copy(out=grouped[:], in_=h2_slots[n][:].rearrange("p t b -> p b t"))
+            h2_grouped[n] = grouped
+
+        def quantise_h2(n):
+            codes = work.tile([P, UNIT_ROWS], U32, name="h2_codes", bufs=4, align_bytes=64)
+            scales = work.tile([P, UNIT_ROWS], U8, name="h2_scales", bufs=4, align_bytes=64)
             nc.vector.quantize_mx(
                 out=codes[:].bitcast(FP8X4),
                 scales=scales[:],
-                in_=h2_grouped[r][:].rearrange("p e b t -> p (e b t)"),
+                in_=h2_grouped[n][:].rearrange("p b t -> p (b t)"),
             )
-            h2_q[r] = (codes, scales)
+            h2_q[n] = (codes, scales)
 
-        def second_layer(r):
-            codes, scales = h2_q[r]
-            sums = psum_acc2.tile([P, D_OUT], F32, name="acc2")
-            for e in range(TREES):
-                cols = slice(e * P, (e + 1) * P)
-                nc.tensor.matmul_mx(
-                    out=sums[:],
-                    lhsT=codes[:, cols].bitcast(FP8X4),
-                    lhsT_scale=scales[:, cols],
-                    rhs=w3[:, e, :].bitcast(FP8X4),
-                    rhs_scale=w3_planes[SCALE_ROWS * e : P, :],
-                    start=(e == 0),
-                    stop=(e == TREES - 1),
-                )
-            acc2[r] = sums
+        def second_layer(c, j):
+            bank = psum_acc2.tile([P, HALF, D_OUT], F32, name="acc2")
+            for ii in range(HALF):
+                cols = slice((HALF * j + ii) * P, (HALF * j + ii + 1) * P)
+                for e in range(TREES):
+                    codes, scales = h2_q[TREES * c + e]
+                    nc.tensor.matmul_mx(
+                        out=bank[:, ii, :],
+                        lhsT=codes[:, cols].bitcast(FP8X4),
+                        lhsT_scale=scales[:, cols],
+                        rhs=w3[:, e, :].bitcast(FP8X4),
+                        rhs_scale=w3_planes[SCALE_ROWS * e : P, :],
+                        start=(e == 0),
+                        stop=(e == TREES - 1),
+                    )
+            acc2[(c, j)] = bank
 
-        def finish(r):
-            result = resident.tile([P, D_OUT], F32, name="out_r%d" % r)
+        def finish(c, j):
+            if j == 0:
+                result[c] = work.tile([P, CHUNK, D_OUT], F32, name="result", bufs=3)
             nc.vector.scalar_tensor_tensor(
-                out=result[:], in0=acc2[r][:], scalar=1.0 / TREES, in1=b3_half[:],
-                op0=MULT, op1=ADD,
+                out=result[c][:, HALF * j : HALF * (j + 1), :], in0=acc2[(c, j)][:],
+                scalar=1.0 / TREES, in1=b3_half[:], op0=MULT, op1=ADD,
             )
-            nc.sync.dma_start(out=out_rows[:, r, :], in_=result[:])
+            if j == CHUNK // HALF - 1:
+                nc.sync.dma_start(
+                    out=out_rows[:, CHUNK * c : CHUNK * (c + 1), :], in_=result[c][:]
+                )
 
-        def live(r):
-            return 0 <= r < ROUNDS
+        def live(n):
+            return 0 <= n < UNITS
 
-        def step(i):
-            if live(i):
-                transpose_h1(i)
-                regroup_h1(i)
-                quantise_h1(i)
-            if live(i - 3):
-                transpose_h2(i - 3)
-                relu_regroup_h2(i - 3)
-            if live(i - 1):
-                first_layer(i - 1)
-                add_bias(i - 1)
-            if live(i - 3):
-                quantise_h2(i - 3)
-            if live(i - 4):
-                second_layer(i - 4)
-                finish(i - 4)
+        def step(s):
+            if live(s - 4):
+                finish(*divmod(s - 4, 2))
+            if live(s - 2):
+                regroup_h2(s - 2)
+            if live(s):
+                transpose_h1(s)
+            if live(s - 2):
+                quantise_h2(s - 2)
+            if live(s):
+                quantise_h1(s)
+            if s == 0:
+                spread_b3()
+                reorder_w2_planes()
+            if s < TREES:
+                for g in range(PASSES1):
+                    reorder_w2(s * PASSES1 + g)
+            if live(s - 1):
+                first_layer(s - 1)
+            if live(s - 3):
+                second_layer(*divmod(s - 3, 2))
+            if live(s + AHEAD):
+                load_h1(s + AHEAD)
 
-        step(0)
-        spread_biases()
-        for i in range(1, ROUNDS + 4):
-            step(i)
+        for s in range(UNITS + 4):
+            step(s)

@@ -28,6 +28,7 @@ UNITS = CHUNKS * TREES
 HALF = CHUNK // 2
 QUADRANT = 32
 SCALE_ROWS = 4
+VECTOR_ROUND = 1
 AHEAD = 6
 
 FLOPS = 2 * TREES * BATCH * (D_H * D_K + D_K * D_OUT)
@@ -141,11 +142,13 @@ def tile_randomforestmlp_pa_t_e_kernel(
         h2_slots, h2_grouped, h2_q = {}, {}, {}
         acc2, result = {}, {}
 
-        def transpose_h1(n):
-            grouped = work.tile(
-                [P, PASSES1, CHUNK, P, PACK], BF16, name="h1_grouped", align_bytes=64
-            )
-            for i in range(CHUNK):
+        def transpose_h1(n, rounds):
+            if n not in h1_grouped:
+                h1_grouped[n] = work.tile(
+                    [P, PASSES1, CHUNK, P, PACK], BF16, name="h1_grouped", align_bytes=64
+                )
+            grouped = h1_grouped[n]
+            for i in rounds:
                 words = h1_sb[(n, i)][:].bitcast(F32)
                 bank = psum_h1t.tile([P, PASSES1, PLANES, P], F32, name="h1t")
                 for g in range(PASSES1):
@@ -157,11 +160,10 @@ def tile_randomforestmlp_pa_t_e_kernel(
                         )
                 dst = grouped[:, :, i].bitcast(F32)
                 src = bank[:].rearrange("p g u b -> p g b u")
-                if i < CHUNK - 1:
-                    nc.scalar.copy(out=dst, in_=src)
-                else:
+                if i == VECTOR_ROUND:
                     nc.vector.tensor_copy(out=dst, in_=src)
-            h1_grouped[n] = grouped
+                else:
+                    nc.scalar.copy(out=dst, in_=src)
 
         def quantise_h1(n):
             codes = work.tile([P, PASSES1 * UNIT_ROWS], U32, name="h1_codes", align_bytes=64)
@@ -173,11 +175,13 @@ def tile_randomforestmlp_pa_t_e_kernel(
             )
             h1_q[n] = (codes, scales)
 
-        def first_layer(n):
+        def first_layer(n, slot_range):
             e = n % TREES
             codes, scales = h1_q[n]
-            slots = work.tile([P, PACK, UNIT_ROWS], BF16, name="h2_slots")
-            for t in range(PACK):
+            if n not in h2_slots:
+                h2_slots[n] = work.tile([P, PACK, UNIT_ROWS], BF16, name="h2_slots")
+            slots = h2_slots[n]
+            for t in slot_range:
                 sums = psum_acc1.tile([P, UNIT_ROWS], F32, name="acc1")
                 chans = slice(t * P, (t + 1) * P)
                 for g in range(PASSES1):
@@ -195,7 +199,6 @@ def tile_randomforestmlp_pa_t_e_kernel(
                 nc.scalar.activation(
                     out=slots[:, t, :], in_=sums[:], func=RELU, bias=b2_cols[:, e, t : t + 1]
                 )
-            h2_slots[n] = slots
 
         def regroup_h2(n):
             grouped = work.tile([P, UNIT_ROWS, PACK], BF16, name="h2_grouped", align_bytes=64)
@@ -250,10 +253,13 @@ def tile_randomforestmlp_pa_t_e_kernel(
             if live(s - 2):
                 regroup_h2(s - 2)
             if live(s):
-                transpose_h1(s)
+                transpose_h1(s, (0, 1))
             if live(s - 2):
                 quantise_h2(s - 2)
+            if live(s - 1):
+                first_layer(s - 1, (0, 1))
             if live(s):
+                transpose_h1(s, (2, 3))
                 quantise_h1(s)
             if s == 0:
                 spread_b3()
@@ -262,7 +268,7 @@ def tile_randomforestmlp_pa_t_e_kernel(
                 for g in range(PASSES1):
                     reorder_w2(s * PASSES1 + g)
             if live(s - 1):
-                first_layer(s - 1)
+                first_layer(s - 1, (2, 3))
             if live(s - 3):
                 second_layer(*divmod(s - 3, 2))
             if live(s + AHEAD):

@@ -206,8 +206,8 @@ def tile_randomforestmlp_pa_t_e_kernel(
             h2_grouped[n] = grouped
 
         def quantise_h2(n):
-            codes = work.tile([P, UNIT_ROWS], U32, name="h2_codes", bufs=4, align_bytes=64)
-            scales = work.tile([P, UNIT_ROWS], U8, name="h2_scales", bufs=4, align_bytes=64)
+            codes = work.tile([P, UNIT_ROWS], U32, name="h2_codes", bufs=5, align_bytes=64)
+            scales = work.tile([P, UNIT_ROWS], U8, name="h2_scales", bufs=5, align_bytes=64)
             nc.vector.quantize_mx(
                 out=codes[:].bitcast(FP8X4),
                 scales=scales[:],
@@ -248,31 +248,32 @@ def tile_randomforestmlp_pa_t_e_kernel(
             return 0 <= n < UNITS
 
         def step(s):
-            if live(s - 4):
-                finish(*divmod(s - 4, 2))
-            if live(s - 2):
-                regroup_h2(s - 2)
+            if live(s - 1):
+                quantise_h1(s - 1)
+            if live(s - 6):
+                finish(*divmod(s - 6, 2))
+            if live(s - 3):
+                regroup_h2(s - 3)
             if live(s):
                 transpose_h1(s, (0, 1))
+            if live(s - 3):
+                quantise_h2(s - 3)
             if live(s - 2):
-                quantise_h2(s - 2)
-            if live(s - 1):
-                first_layer(s - 1, (0, 1))
+                first_layer(s - 2, (0, 1))
             if live(s):
                 transpose_h1(s, (2, 3))
-                quantise_h1(s)
             if s == 0:
                 spread_b3()
                 reorder_w2_planes()
             if s < TREES:
                 for g in range(PASSES1):
                     reorder_w2(s * PASSES1 + g)
-            if live(s - 1):
-                first_layer(s - 1, (2, 3))
-            if live(s - 3):
-                second_layer(*divmod(s - 3, 2))
+            if live(s - 2):
+                first_layer(s - 2, (2, 3))
+            if live(s - 5):
+                second_layer(*divmod(s - 5, 2))
             if live(s + AHEAD):
                 load_h1(s + AHEAD)
 
-        for s in range(UNITS + 4):
+        for s in range(UNITS + 6):
             step(s)

@@ -29,6 +29,7 @@ HALF = CHUNK // 2
 QUADRANT = 32
 SCALE_ROWS = 4
 VECTOR_ROUND = 1
+WHOLE_UNIT = slice(0, UNIT_ROWS)
 AHEAD = 6
 
 FLOPS = 2 * TREES * BATCH * (D_H * D_K + D_K * D_OUT)
@@ -140,7 +141,7 @@ def tile_randomforestmlp_pa_t_e_kernel(
 
         h1_grouped, h1_q = {}, {}
         h2_slots, h2_grouped, h2_q = {}, {}, {}
-        acc2, result = {}, {}
+        acc2 = {}
 
         def transpose_h1(n, rounds):
             if n not in h1_grouped:
@@ -175,18 +176,18 @@ def tile_randomforestmlp_pa_t_e_kernel(
             )
             h1_q[n] = (codes, scales)
 
-        def first_layer(n, slot_range):
+        def first_layer(n, slot_range, rows=WHOLE_UNIT):
             e = n % TREES
             codes, scales = h1_q[n]
             if n not in h2_slots:
                 h2_slots[n] = work.tile([P, PACK, UNIT_ROWS], BF16, name="h2_slots")
             slots = h2_slots[n]
             for t in slot_range:
-                sums = psum_acc1.tile([P, UNIT_ROWS], F32, name="acc1")
+                sums = psum_acc1.tile([P, rows.stop - rows.start], F32, name="acc1")
                 chans = slice(t * P, (t + 1) * P)
                 for g in range(PASSES1):
                     w = e * PASSES1 + g
-                    cols = slice(g * UNIT_ROWS, (g + 1) * UNIT_ROWS)
+                    cols = slice(g * UNIT_ROWS + rows.start, g * UNIT_ROWS + rows.stop)
                     nc.tensor.matmul_mx(
                         out=sums[:],
                         lhsT=w2[:, w, chans].bitcast(FP8X4),
@@ -197,26 +198,34 @@ def tile_randomforestmlp_pa_t_e_kernel(
                         stop=(g == PASSES1 - 1),
                     )
                 nc.scalar.activation(
-                    out=slots[:, t, :], in_=sums[:], func=RELU, bias=b2_cols[:, e, t : t + 1]
+                    out=slots[:, t, rows], in_=sums[:], func=RELU, bias=b2_cols[:, e, t : t + 1]
                 )
 
-        def regroup_h2(n):
-            grouped = work.tile([P, UNIT_ROWS, PACK], BF16, name="h2_grouped", align_bytes=64)
-            nc.vector.tensor_copy(out=grouped[:], in_=h2_slots[n][:].rearrange("p t b -> p b t"))
-            h2_grouped[n] = grouped
-
-        def quantise_h2(n):
-            codes = work.tile([P, UNIT_ROWS], U32, name="h2_codes", bufs=5, align_bytes=64)
-            scales = work.tile([P, UNIT_ROWS], U8, name="h2_scales", bufs=5, align_bytes=64)
-            nc.vector.quantize_mx(
-                out=codes[:].bitcast(FP8X4),
-                scales=scales[:],
-                in_=h2_grouped[n][:].rearrange("p b t -> p (b t)"),
+        def regroup_h2(n, rows=WHOLE_UNIT):
+            if n not in h2_grouped:
+                h2_grouped[n] = work.tile(
+                    [P, UNIT_ROWS, PACK], BF16, name="h2_grouped", align_bytes=64
+                )
+            nc.vector.tensor_copy(
+                out=h2_grouped[n][:, rows, :],
+                in_=h2_slots[n][:, :, rows].rearrange("p t b -> p b t"),
             )
-            h2_q[n] = (codes, scales)
 
-        def second_layer(c, j):
-            bank = psum_acc2.tile([P, HALF, D_OUT], F32, name="acc2")
+        def quantise_h2(n, rows=WHOLE_UNIT):
+            if n not in h2_q:
+                h2_q[n] = (
+                    work.tile([P, UNIT_ROWS], U32, name="h2_codes", bufs=5, align_bytes=64),
+                    work.tile([P, UNIT_ROWS], U8, name="h2_scales", bufs=5, align_bytes=64),
+                )
+            codes, scales = h2_q[n]
+            nc.vector.quantize_mx(
+                out=codes[:, rows].bitcast(FP8X4),
+                scales=scales[:, rows],
+                in_=h2_grouped[n][:, rows, :].rearrange("p b t -> p (b t)"),
+            )
+
+        def second_layer(c, j, pool, tag):
+            bank = pool.tile([P, HALF, D_OUT], F32, name=tag)
             for ii in range(HALF):
                 cols = slice((HALF * j + ii) * P, (HALF * j + ii + 1) * P)
                 for e in range(TREES):
@@ -233,16 +242,13 @@ def tile_randomforestmlp_pa_t_e_kernel(
             acc2[(c, j)] = bank
 
         def finish(c, j):
-            if j == 0:
-                result[c] = work.tile([P, CHUNK, D_OUT], F32, name="result", bufs=3)
+            result = work.tile([P, HALF, D_OUT], F32, name="result", bufs=6)
             nc.vector.scalar_tensor_tensor(
-                out=result[c][:, HALF * j : HALF * (j + 1), :], in0=acc2[(c, j)][:],
+                out=result[:], in0=acc2[(c, j)][:],
                 scalar=1.0 / TREES, in1=b3_half[:], op0=MULT, op1=ADD,
             )
-            if j == CHUNK // HALF - 1:
-                nc.sync.dma_start(
-                    out=out_rows[:, CHUNK * c : CHUNK * (c + 1), :], in_=result[c][:]
-                )
+            first = CHUNK * c + HALF * j
+            nc.sync.dma_start(out=out_rows[:, first : first + HALF, :], in_=result[:])
 
         def live(n):
             return 0 <= n < UNITS
@@ -271,9 +277,27 @@ def tile_randomforestmlp_pa_t_e_kernel(
             if live(s - 2):
                 first_layer(s - 2, (2, 3))
             if live(s - 5):
-                second_layer(*divmod(s - 5, 2))
+                second_layer(*divmod(s - 5, 2), psum_acc2, "acc2")
             if live(s + AHEAD):
                 load_h1(s + AHEAD)
 
-        for s in range(UNITS + 6):
+        for s in range(UNITS + 1):
             step(s)
+
+        last = UNITS - 1
+        end_c = CHUNKS - 1
+        halves = [slice(j * HALF * P, (j + 1) * HALF * P) for j in range(CHUNK // HALF)]
+        finish(end_c - 2, 1)
+        for rows in halves:
+            first_layer(last, range(PACK), rows)
+        regroup_h2(last - 1)
+        quantise_h2(last - 1)
+        second_layer(end_c - 1, 0, psum_acc2, "acc2")
+        second_layer(end_c - 1, 1, psum_h1t, "h1t")
+        for j, rows in enumerate(halves):
+            regroup_h2(last, rows)
+            quantise_h2(last, rows)
+            finish(end_c - 1, j)
+            second_layer(end_c, j, psum_h1t, "h1t")
+        for j in range(CHUNK // HALF):
+            finish(end_c, j)

@@ -28,7 +28,7 @@ UNITS = CHUNKS * TREES
 HALF = CHUNK // 2
 QUADRANT = 32
 SCALE_ROWS = 4
-VECTOR_ROUND = 1
+SPLIT = 2
 WHOLE_UNIT = slice(0, UNIT_ROWS)
 AHEAD = 6
 
@@ -45,7 +45,7 @@ def tile_randomforestmlp_pa_t_e_kernel(
     with ExitStack() as ctx:
         ctx.enter_context(tc.manual_schedule())
         consts = ctx.enter_context(tc.tile_pool(name="consts", bufs=1))
-        h1_pool = ctx.enter_context(tc.tile_pool(name="h1_pool", bufs=(AHEAD + 1) * CHUNK))
+        h1_pool = ctx.enter_context(tc.tile_pool(name="h1_pool", bufs=AHEAD + 1))
         work = ctx.enter_context(tc.tile_pool(name="work", bufs=2))
         psum_h1t = ctx.enter_context(tc.psum_pool(name="psum_h1t", bufs=3))
         psum_acc1 = ctx.enter_context(tc.psum_pool(name="psum_acc1", bufs=4))
@@ -84,10 +84,12 @@ def tile_randomforestmlp_pa_t_e_kernel(
 
         def load_h1(n):
             c, e = divmod(n, TREES)
+            x = h1_pool.tile([P, CHUNK * D_H], BF16, name="h1_sb")
             for i in range(CHUNK):
-                x = h1_pool.tile([P, D_H], BF16, name="h1_sb")
-                nc.sync.dma_start(out=x[:], in_=h1_rows[e][:, CHUNK * c + i, :])
-                h1_sb[(n, i)] = x
+                nc.sync.dma_start(
+                    out=x[:, i * D_H : (i + 1) * D_H], in_=h1_rows[e][:, CHUNK * c + i, :]
+                )
+            h1_sb[n] = x
 
         def load_planes(planes_sb, scales):
             passes = scales.shape[0]
@@ -139,9 +141,19 @@ def tile_randomforestmlp_pa_t_e_kernel(
             )
             nc.vector.tensor_scalar_mul(out=b3_half[:], in0=spread[:], scalar1=1.0 / TREES)
 
-        h1_grouped, h1_q = {}, {}
+        h1_planes, h1_grouped, h1_q = {}, {}, {}
         h2_slots, h2_grouped, h2_q = {}, {}, {}
         acc2 = {}
+
+        def split_planes(n):
+            planes = work.tile([P, SPLIT * PASSES1, PLANES, P], F32, name="h1_planes")
+            nc.vector.tensor_copy(
+                out=planes[:],
+                in_=h1_sb[n][:, 0 : SPLIT * D_H]
+                .bitcast(F32)
+                .rearrange("p (a m u) -> p a u m", m=P, u=PLANES),
+            )
+            h1_planes[n] = planes
 
         def transpose_h1(n, rounds):
             if n not in h1_grouped:
@@ -150,21 +162,19 @@ def tile_randomforestmlp_pa_t_e_kernel(
                 )
             grouped = h1_grouped[n]
             for i in rounds:
-                words = h1_sb[(n, i)][:].bitcast(F32)
+                words = h1_sb[n][:, i * D_H : (i + 1) * D_H].bitcast(F32)
                 bank = psum_h1t.tile([P, PASSES1, PLANES, P], F32, name="h1t")
                 for g in range(PASSES1):
                     for u in range(PLANES):
-                        nc.tensor.transpose(
-                            bank[:, g, u, :],
-                            words[:, WORDS_PASS * g + u : WORDS_PASS * (g + 1) : PLANES],
-                            ident[:],
-                        )
-                dst = grouped[:, :, i].bitcast(F32)
-                src = bank[:].rearrange("p g u b -> p g b u")
-                if i == VECTOR_ROUND:
-                    nc.vector.tensor_copy(out=dst, in_=src)
-                else:
-                    nc.scalar.copy(out=dst, in_=src)
+                        if n in h1_planes and i < SPLIT:
+                            plane = h1_planes[n][:, i * PASSES1 + g, u, :]
+                        else:
+                            plane = words[:, WORDS_PASS * g + u : WORDS_PASS * (g + 1) : PLANES]
+                        nc.tensor.transpose(bank[:, g, u, :], plane, ident[:])
+                nc.scalar.copy(
+                    out=grouped[:, :, i].bitcast(F32),
+                    in_=bank[:].rearrange("p g u b -> p g b u"),
+                )
 
         def quantise_h1(n):
             codes = work.tile([P, PASSES1 * UNIT_ROWS], U32, name="h1_codes", align_bytes=64)
@@ -260,10 +270,12 @@ def tile_randomforestmlp_pa_t_e_kernel(
                 finish(*divmod(s - 6, 2))
             if live(s - 3):
                 regroup_h2(s - 3)
-            if live(s):
-                transpose_h1(s, (0, 1))
+            if live(s + 1):
+                split_planes(s + 1)
             if live(s - 3):
                 quantise_h2(s - 3)
+            if live(s):
+                transpose_h1(s, (0, 1))
             if live(s - 2):
                 first_layer(s - 2, (0, 1))
             if live(s):

@@ -29,6 +29,7 @@ HALF = CHUNK // 2
 QUADRANT = 32
 SCALE_ROWS = 4
 SPLIT = 2
+RUN = 4
 WHOLE_UNIT = slice(0, UNIT_ROWS)
 AHEAD = 6
 
@@ -217,8 +218,8 @@ def tile_randomforestmlp_pa_t_e_kernel(
                     [P, UNIT_ROWS, PACK], BF16, name="h2_grouped", align_bytes=64
                 )
             nc.vector.tensor_copy(
-                out=h2_grouped[n][:, rows, :],
-                in_=h2_slots[n][:, :, rows].rearrange("p t b -> p b t"),
+                out=h2_grouped[n][:, rows, :].rearrange("p (c i) t -> p c t i", i=RUN),
+                in_=h2_slots[n][:, :, rows].rearrange("p t (c i) -> p c t i", i=RUN),
             )
 
         def quantise_h2(n, rows=WHOLE_UNIT):

@@ -29,6 +29,9 @@ HALF = CHUNK // 2
 QUADRANT = 32
 SCALE_ROWS = 4
 SPLIT = 2
+FIRST_LAYER_LAG = 2
+BUSY_FIRST = 4
+BUSY_BETWEEN = 3
 RUN = 4
 WHOLE_UNIT = slice(0, UNIT_ROWS)
 AHEAD = 6
@@ -75,6 +78,8 @@ def tile_randomforestmlp_pa_t_e_kernel(
         ones = consts.tile([P, P], BF16, name="ones")
         b3_rows = consts.tile([P, HALF, D_OUT], BF16, name="b3_rows")
         nc.vector.memset(ones[:], 1.0)
+        zeros = consts.tile([P, UNIT_ROWS], BF16, name="zeros")
+        nc.vector.memset(zeros[:], 0.0)
         nc.vector.memset(b3_rows[:], 0.0)
         for j in range(HALF):
             nc.scalar.dma_start(out=b3_rows[0:TREES, j, :], in_=b3)
@@ -131,6 +136,11 @@ def tile_randomforestmlp_pa_t_e_kernel(
                 out=w2[:, w, :].bitcast(I32).rearrange("p (t m) -> p t m", t=PACK),
                 in_=w2_raw[:, w, :].bitcast(I32).rearrange("p (m t) -> p t m", t=PACK),
             )
+
+        def keep_busy(count):
+            for i in range(count):
+                unread = psum_acc1.tile([P, UNIT_ROWS], F32, name="acc1")
+                nc.tensor.matmul(out=unread[:], lhsT=ones[:], rhs=zeros[:], start=True, stop=True)
 
         def spread_b3():
             spread = psum_acc2.tile([P, HALF, D_OUT], F32, name="acc2")
@@ -281,6 +291,8 @@ def tile_randomforestmlp_pa_t_e_kernel(
                 first_layer(s - 2, (0, 1))
             if live(s):
                 transpose_h1(s, (2, 3))
+            if s < FIRST_LAYER_LAG:
+                keep_busy(BUSY_BETWEEN)
             if s == 0:
                 spread_b3()
                 reorder_w2_planes()
@@ -294,6 +306,7 @@ def tile_randomforestmlp_pa_t_e_kernel(
             if live(s + AHEAD):
                 load_h1(s + AHEAD)
 
+        keep_busy(BUSY_FIRST)
         for s in range(UNITS + 1):
             step(s)
 

@@ -29,6 +29,7 @@ HALF = CHUNK // 2
 QUADRANT = 32
 SCALE_ROWS = 4
 SPLIT = 2
+FIRST_SPLIT = 3
 FIRST_LAYER_LAG = 2
 BUSY_FIRST = 4
 BUSY_BETWEEN = 3
@@ -117,12 +118,14 @@ def tile_randomforestmlp_pa_t_e_kernel(
         load_words(w2_raw, W2_words, 0)
         load_words(w2_raw, W2_words, 1)
         load_h1(1)
+        load_h1(2)
         load_words(w2_raw, W2_words, 2)
         load_words(w2_raw, W2_words, 3)
+        load_h1(3)
         load_planes(w3_planes, W3_scales)
         load_words(w3, W3_words, 0)
         load_words(w3, W3_words, 1)
-        for n in range(2, AHEAD):
+        for n in range(4, AHEAD):
             load_h1(n)
 
         def reorder_w2_planes():
@@ -281,7 +284,7 @@ def tile_randomforestmlp_pa_t_e_kernel(
                 finish(*divmod(s - 6, 2))
             if live(s - 3):
                 regroup_h2(s - 3)
-            if live(s + 1):
+            if live(s + 1) and s + 1 >= FIRST_SPLIT:
                 split_planes(s + 1)
             if live(s - 3):
                 quantise_h2(s - 3)

@@ -56,6 +56,11 @@ def tile_randomforestmlp_pa_t_e_kernel(
         psum_acc1 = ctx.enter_context(tc.psum_pool(name="psum_acc1", bufs=4))
         psum_acc2 = ctx.enter_context(tc.psum_pool(name="psum_acc2", bufs=1))
 
+        ones = consts.tile([P, P], BF16, name="ones")
+        zeros = consts.tile([P, UNIT_ROWS], BF16, name="zeros")
+        nc.vector.memset(ones[:], 1.0)
+        nc.vector.memset(zeros[:], 0.0)
+
         ident = consts.tile([P, P], F32, name="ident")
         make_identity(nc, ident[:])
 
@@ -76,11 +81,7 @@ def tile_randomforestmlp_pa_t_e_kernel(
         b2_cols = consts.tile([P, TREES, PACK], F32, name="b2_cols")
         nc.scalar.dma_start(out=b2_cols_bf[:], in_=b2.rearrange("e (p t) -> p e t", t=PACK))
 
-        ones = consts.tile([P, P], BF16, name="ones")
         b3_rows = consts.tile([P, HALF, D_OUT], BF16, name="b3_rows")
-        nc.vector.memset(ones[:], 1.0)
-        zeros = consts.tile([P, UNIT_ROWS], BF16, name="zeros")
-        nc.vector.memset(zeros[:], 0.0)
         nc.vector.memset(b3_rows[:], 0.0)
         for j in range(HALF):
             nc.scalar.dma_start(out=b3_rows[0:TREES, j, :], in_=b3)

@@ -115,10 +115,10 @@ def tile_randomforestmlp_pa_t_e_kernel(
             )
 
         load_h1(0)
+        load_h1(1)
         load_planes(w2_planes_raw, W2_scales)
         load_words(w2_raw, W2_words, 0)
         load_words(w2_raw, W2_words, 1)
-        load_h1(1)
         load_h1(2)
         load_words(w2_raw, W2_words, 2)
         load_words(w2_raw, W2_words, 3)
@@ -226,12 +226,12 @@ def tile_randomforestmlp_pa_t_e_kernel(
                     out=slots[:, t, rows], in_=sums[:], func=RELU, bias=b2_cols[:, e, t : t + 1]
                 )
 
-        def regroup_h2(n, rows=WHOLE_UNIT):
+        def regroup_h2(n, rows=WHOLE_UNIT, copy=nc.vector.tensor_copy):
             if n not in h2_grouped:
                 h2_grouped[n] = work.tile(
                     [P, UNIT_ROWS, PACK], BF16, name="h2_grouped", align_bytes=64
                 )
-            nc.vector.tensor_copy(
+            copy(
                 out=h2_grouped[n][:, rows, :].rearrange("p (c i) t -> p c t i", i=RUN),
                 in_=h2_slots[n][:, :, rows].rearrange("p t (c i) -> p c t i", i=RUN),
             )
@@ -281,6 +281,11 @@ def tile_randomforestmlp_pa_t_e_kernel(
         def step(s):
             if live(s - 1):
                 quantise_h1(s - 1)
+            if s == 1:
+                reorder_w2_planes()
+            if 1 <= s <= TREES:
+                for g in range(PASSES1):
+                    reorder_w2((s - 1) * PASSES1 + g)
             if live(s - 6):
                 finish(*divmod(s - 6, 2))
             if live(s - 3):
@@ -299,10 +304,6 @@ def tile_randomforestmlp_pa_t_e_kernel(
                 keep_busy(BUSY_BETWEEN)
             if s == 0:
                 spread_b3()
-                reorder_w2_planes()
-            if s < TREES:
-                for g in range(PASSES1):
-                    reorder_w2(s * PASSES1 + g)
             if live(s - 2):
                 first_layer(s - 2, (2, 3))
             if live(s - 5):
@@ -325,9 +326,10 @@ def tile_randomforestmlp_pa_t_e_kernel(
         second_layer(end_c - 1, 0, psum_acc2, "acc2")
         second_layer(end_c - 1, 1, psum_h1t, "h1t")
         for j, rows in enumerate(halves):
-            regroup_h2(last, rows)
+            regroup_h2(last, rows, nc.vector.tensor_copy if j == 0 else nc.scalar.copy)
+        for j, rows in enumerate(halves):
             quantise_h2(last, rows)
-            finish(end_c - 1, j)
             second_layer(end_c, j, psum_h1t, "h1t")
+            finish(end_c - 1, j)
         for j in range(CHUNK // HALF):
             finish(end_c, j)

@@ -28,7 +28,7 @@ UNITS = CHUNKS * TREES
 HALF = CHUNK // 2
 QUADRANT = 32
 SCALE_ROWS = 4
-SPLIT = 2
+SPLIT = 3
 FIRST_SPLIT = 3
 FIRST_LAYER_LAG = 2
 BUSY_FIRST = 4
@@ -52,9 +52,8 @@ def tile_randomforestmlp_pa_t_e_kernel(
         consts = ctx.enter_context(tc.tile_pool(name="consts", bufs=1))
         h1_pool = ctx.enter_context(tc.tile_pool(name="h1_pool", bufs=AHEAD + 1))
         work = ctx.enter_context(tc.tile_pool(name="work", bufs=2))
-        psum_h1t = ctx.enter_context(tc.psum_pool(name="psum_h1t", bufs=3))
+        psum_h1t = ctx.enter_context(tc.psum_pool(name="psum_h1t", bufs=4))
         psum_acc1 = ctx.enter_context(tc.psum_pool(name="psum_acc1", bufs=4))
-        psum_acc2 = ctx.enter_context(tc.psum_pool(name="psum_acc2", bufs=1))
 
         ones = consts.tile([P, P], BF16, name="ones")
         zeros = consts.tile([P, UNIT_ROWS], BF16, name="zeros")
@@ -147,7 +146,7 @@ def tile_randomforestmlp_pa_t_e_kernel(
                 nc.tensor.matmul(out=unread[:], lhsT=ones[:], rhs=zeros[:], start=True, stop=True)
 
         def spread_b3():
-            spread = psum_acc2.tile([P, HALF, D_OUT], F32, name="acc2")
+            spread = psum_acc1.tile([P, HALF, D_OUT], F32, name="acc1")
             nc.tensor.matmul(
                 out=spread[:].rearrange("p j n -> p (j n)"),
                 lhsT=ones[:],
@@ -295,19 +294,15 @@ def tile_randomforestmlp_pa_t_e_kernel(
             if live(s - 3):
                 quantise_h2(s - 3)
             if live(s):
-                transpose_h1(s, (0, 1))
-            if live(s - 2):
-                first_layer(s - 2, (0, 1))
-            if live(s):
-                transpose_h1(s, (2, 3))
+                transpose_h1(s, range(CHUNK))
             if s < FIRST_LAYER_LAG:
                 keep_busy(BUSY_BETWEEN)
             if s == 0:
                 spread_b3()
             if live(s - 2):
-                first_layer(s - 2, (2, 3))
+                first_layer(s - 2, range(PACK))
             if live(s - 5):
-                second_layer(*divmod(s - 5, 2), psum_acc2, "acc2")
+                second_layer(*divmod(s - 5, 2), psum_acc1, "acc1")
             if live(s + AHEAD):
                 load_h1(s + AHEAD)
 
@@ -323,7 +318,7 @@ def tile_randomforestmlp_pa_t_e_kernel(
             first_layer(last, range(PACK), rows)
         regroup_h2(last - 1)
         quantise_h2(last - 1)
-        second_layer(end_c - 1, 0, psum_acc2, "acc2")
+        second_layer(end_c - 1, 0, psum_acc1, "acc1")
         second_layer(end_c - 1, 1, psum_h1t, "h1t")
         for j, rows in enumerate(halves):
             regroup_h2(last, rows, nc.vector.tensor_copy if j == 0 else nc.scalar.copy)

@@ -51,7 +51,7 @@ def tile_randomforestmlp_pa_t_e_kernel(
         ctx.enter_context(tc.manual_schedule())
         consts = ctx.enter_context(tc.tile_pool(name="consts", bufs=1))
         h1_pool = ctx.enter_context(tc.tile_pool(name="h1_pool", bufs=AHEAD + 1))
-        work = ctx.enter_context(tc.tile_pool(name="work", bufs=2))
+        work = ctx.enter_context(tc.tile_pool(name="work", bufs=3))
         psum_h1t = ctx.enter_context(tc.psum_pool(name="psum_h1t", bufs=4))
         psum_acc1 = ctx.enter_context(tc.psum_pool(name="psum_acc1", bufs=4))
 
@@ -190,24 +190,37 @@ def tile_randomforestmlp_pa_t_e_kernel(
                     in_=bank[:].rearrange("p g u b -> p g b u"),
                 )
 
-        def quantise_h1(n):
-            codes = work.tile([P, PASSES1 * UNIT_ROWS], U32, name="h1_codes", align_bytes=64)
-            scales = work.tile([P, PASSES1 * UNIT_ROWS], U8, name="h1_scales", align_bytes=64)
-            nc.vector.quantize_mx(
-                out=codes[:].bitcast(FP8X4),
-                scales=scales[:],
-                in_=h1_grouped[n][:].rearrange("p g i b t -> p (g i b t)"),
-            )
-            h1_q[n] = (codes, scales)
+        def quantise_h1(n, rows=WHOLE_UNIT):
+            if n not in h1_q:
+                h1_q[n] = (
+                    work.tile([P, PASSES1 * UNIT_ROWS], U32, name="h1_codes", align_bytes=64),
+                    work.tile([P, PASSES1 * UNIT_ROWS], U8, name="h1_scales", align_bytes=64),
+                )
+            codes, scales = h1_q[n]
+            if rows == WHOLE_UNIT:
+                nc.vector.quantize_mx(
+                    out=codes[:].bitcast(FP8X4),
+                    scales=scales[:],
+                    in_=h1_grouped[n][:].rearrange("p g i b t -> p (g i b t)"),
+                )
+                return
+            rounds = slice(rows.start // P, rows.stop // P)
+            for g in range(PASSES1):
+                cols = slice(g * UNIT_ROWS + rows.start, g * UNIT_ROWS + rows.stop)
+                nc.vector.quantize_mx(
+                    out=codes[:, cols].bitcast(FP8X4),
+                    scales=scales[:, cols],
+                    in_=h1_grouped[n][:, g, rounds].rearrange("p i b t -> p (i b t)"),
+                )
 
-        def first_layer(n, slot_range, rows=WHOLE_UNIT):
+        def first_layer(n, slot_range, rows=WHOLE_UNIT, pool=psum_acc1, tag="acc1"):
             e = n % TREES
             codes, scales = h1_q[n]
             if n not in h2_slots:
                 h2_slots[n] = work.tile([P, PACK, UNIT_ROWS], BF16, name="h2_slots")
             slots = h2_slots[n]
             for t in slot_range:
-                sums = psum_acc1.tile([P, rows.stop - rows.start], F32, name="acc1")
+                sums = pool.tile([P, rows.stop - rows.start], F32, name=tag)
                 chans = slice(t * P, (t + 1) * P)
                 for g in range(PASSES1):
                     w = e * PASSES1 + g
@@ -277,54 +290,58 @@ def tile_randomforestmlp_pa_t_e_kernel(
         def live(n):
             return 0 <= n < UNITS
 
+        halves = [slice(j * HALF * P, (j + 1) * HALF * P) for j in range(CHUNK // HALF)]
+
         def step(s):
-            if live(s - 1):
-                quantise_h1(s - 1)
-            if s == 1:
-                reorder_w2_planes()
-            if 1 <= s <= TREES:
-                for g in range(PASSES1):
-                    reorder_w2((s - 1) * PASSES1 + g)
-            if live(s - 6):
-                finish(*divmod(s - 6, 2))
-            if live(s - 3):
-                regroup_h2(s - 3)
+            if live(s - 5):
+                finish(*divmod(s - 5, 2))
             if live(s + 1) and s + 1 >= FIRST_SPLIT:
                 split_planes(s + 1)
-            if live(s - 3):
-                quantise_h2(s - 3)
-            if live(s):
-                transpose_h1(s, range(CHUNK))
-            if s < FIRST_LAYER_LAG:
-                keep_busy(BUSY_BETWEEN)
-            if s == 0:
-                spread_b3()
             if live(s - 2):
-                first_layer(s - 2, range(PACK))
-            if live(s - 5):
-                second_layer(*divmod(s - 5, 2), psum_acc1, "acc1")
+                regroup_h2(s - 2)
+            transpose_h1(s, range(CHUNK))
+            if live(s - 4):
+                second_layer(*divmod(s - 4, 2), psum_acc1, "acc1")
+            if s == 0:
+                keep_busy(BUSY_BETWEEN)
+                spread_b3()
+            if live(s - 1):
+                first_layer(s - 1, range(PACK))
+            if s < UNITS - 1:
+                quantise_h1(s)
+            else:
+                for rows in halves:
+                    quantise_h1(s, rows)
+            if live(s - 2):
+                quantise_h2(s - 2)
+            if s == 0:
+                reorder_w2_planes()
+            if s < TREES:
+                for g in range(PASSES1):
+                    reorder_w2(s * PASSES1 + g)
             if live(s + AHEAD):
                 load_h1(s + AHEAD)
 
         keep_busy(BUSY_FIRST)
-        for s in range(UNITS + 1):
+        for s in range(UNITS):
             step(s)
 
         last = UNITS - 1
         end_c = CHUNKS - 1
-        halves = [slice(j * HALF * P, (j + 1) * HALF * P) for j in range(CHUNK // HALF)]
         finish(end_c - 2, 1)
-        for rows in halves:
-            first_layer(last, range(PACK), rows)
-        regroup_h2(last - 1)
-        quantise_h2(last - 1)
-        second_layer(end_c - 1, 0, psum_acc1, "acc1")
+        first_layer(last, range(PACK), halves[0], psum_h1t, "h1t")
+        first_layer(last, range(PACK), halves[1])
+        second_layer(end_c - 1, 0, psum_h1t, "h1t")
         second_layer(end_c - 1, 1, psum_h1t, "h1t")
-        for j, rows in enumerate(halves):
-            regroup_h2(last, rows, nc.vector.tensor_copy if j == 0 else nc.scalar.copy)
-        for j, rows in enumerate(halves):
-            quantise_h2(last, rows)
-            second_layer(end_c, j, psum_h1t, "h1t")
-            finish(end_c - 1, j)
+        regroup_h2(last - 1)
+        regroup_h2(last, halves[0])
+        regroup_h2(last, halves[1], nc.scalar.copy)
+        quantise_h2(last - 1)
+        quantise_h2(last, halves[0])
+        second_layer(end_c, 0, psum_h1t, "h1t")
+        finish(end_c - 1, 0)
+        quantise_h2(last, halves[1])
+        second_layer(end_c, 1, psum_h1t, "h1t")
+        finish(end_c - 1, 1)
         for j in range(CHUNK // HALF):
             finish(end_c, j)

@@ -28,7 +28,7 @@ UNITS = CHUNKS * TREES
 HALF = CHUNK // 2
 QUADRANT = 32
 SCALE_ROWS = 4
-SPLIT = 3
+SPLIT = 7
 FIRST_SPLIT = 3
 FIRST_LAYER_LAG = 2
 BUSY_FIRST = 4
@@ -160,12 +160,12 @@ def tile_randomforestmlp_pa_t_e_kernel(
         acc2 = {}
 
         def split_planes(n):
-            planes = work.tile([P, SPLIT * PASSES1, PLANES, P], F32, name="h1_planes")
+            planes = work.tile([P, PLANES, SPLIT, P], F32, name="h1_planes")
             nc.vector.tensor_copy(
                 out=planes[:],
-                in_=h1_sb[n][:, 0 : SPLIT * D_H]
+                in_=h1_sb[n][:, 0 : SPLIT * K_PASS]
                 .bitcast(F32)
-                .rearrange("p (a m u) -> p a u m", m=P, u=PLANES),
+                .rearrange("p (a m u) -> p u a m", m=P, u=PLANES),
             )
             h1_planes[n] = planes
 
@@ -180,8 +180,8 @@ def tile_randomforestmlp_pa_t_e_kernel(
                 bank = psum_h1t.tile([P, PASSES1, PLANES, P], F32, name="h1t")
                 for g in range(PASSES1):
                     for u in range(PLANES):
-                        if n in h1_planes and i < SPLIT:
-                            plane = h1_planes[n][:, i * PASSES1 + g, u, :]
+                        if n in h1_planes and i * PASSES1 + g < SPLIT:
+                            plane = h1_planes[n][:, u, i * PASSES1 + g, :]
                         else:
                             plane = words[:, WORDS_PASS * g + u : WORDS_PASS * (g + 1) : PLANES]
                         nc.tensor.transpose(bank[:, g, u, :], plane, ident[:])

@@ -29,12 +29,13 @@ HALF = CHUNK // 2
 QUADRANT = 32
 SCALE_ROWS = 4
 SPLIT = 7
-FIRST_SPLIT = 3
+FIRST_SPLIT = 4
 FIRST_LAYER_LAG = 2
 BUSY_FIRST = 4
 BUSY_BETWEEN = 3
 RUN = 4
 WHOLE_UNIT = slice(0, UNIT_ROWS)
+ONE_LOAD = 3
 AHEAD = 6
 
 FLOPS = 2 * TREES * BATCH * (D_H * D_K + D_K * D_OUT)
@@ -89,14 +90,21 @@ def tile_randomforestmlp_pa_t_e_kernel(
 
         h1_sb = {}
 
-        def load_h1(n):
+        def load_h1(n, rounds=range(CHUNK)):
             c, e = divmod(n, TREES)
-            x = h1_pool.tile([P, CHUNK * D_H], BF16, name="h1_sb")
-            for i in range(CHUNK):
+            if n not in h1_sb:
+                h1_sb[n] = h1_pool.tile([P, CHUNK * D_H], BF16, name="h1_sb")
+            x = h1_sb[n]
+            if n >= ONE_LOAD:
+                nc.sync.dma_start(
+                    out=x[:],
+                    in_=h1_rows[e][:, CHUNK * c : CHUNK * (c + 1), :].rearrange("p r k -> p (r k)"),
+                )
+                return
+            for i in rounds:
                 nc.sync.dma_start(
                     out=x[:, i * D_H : (i + 1) * D_H], in_=h1_rows[e][:, CHUNK * c + i, :]
                 )
-            h1_sb[n] = x
 
         def load_planes(planes_sb, scales):
             passes = scales.shape[0]
@@ -122,10 +130,11 @@ def tile_randomforestmlp_pa_t_e_kernel(
         load_words(w2_raw, W2_words, 2)
         load_words(w2_raw, W2_words, 3)
         load_h1(3)
+        load_h1(4)
         load_planes(w3_planes, W3_scales)
         load_words(w3, W3_words, 0)
         load_words(w3, W3_words, 1)
-        for n in range(4, AHEAD):
+        for n in range(5, AHEAD):
             load_h1(n)
 
         def reorder_w2_planes():
@@ -153,7 +162,7 @@ def tile_randomforestmlp_pa_t_e_kernel(
                 rhs=b3_rows[:].rearrange("p j n -> p (j n)"),
                 start=True, stop=True,
             )
-            nc.vector.tensor_scalar_mul(out=b3_half[:], in0=spread[:], scalar1=1.0 / TREES)
+            nc.scalar.mul(out=b3_half[:], in_=spread[:], mul=1.0 / TREES)
 
         h1_planes, h1_grouped, h1_q = {}, {}, {}
         h2_slots, h2_grouped, h2_q = {}, {}, {}
@@ -300,23 +309,27 @@ def tile_randomforestmlp_pa_t_e_kernel(
             if live(s - 2):
                 regroup_h2(s - 2)
             transpose_h1(s, range(CHUNK))
-            if live(s - 4):
-                second_layer(*divmod(s - 4, 2), psum_acc1, "acc1")
             if s == 0:
-                keep_busy(BUSY_BETWEEN)
+                keep_busy(2)
                 spread_b3()
             if live(s - 1):
                 first_layer(s - 1, range(PACK))
-            if s < UNITS - 1:
+            if live(s - 4):
+                second_layer(*divmod(s - 4, 2), psum_acc1, "acc1")
+            if s == 0:
+                for rows in halves:
+                    quantise_h1(s, rows)
+                reorder_w2_planes()
+                reorder_w2(0)
+                reorder_w2(1)
+            elif s < UNITS - 1:
                 quantise_h1(s)
             else:
                 for rows in halves:
                     quantise_h1(s, rows)
             if live(s - 2):
                 quantise_h2(s - 2)
-            if s == 0:
-                reorder_w2_planes()
-            if s < TREES:
+            if s == 1:
                 for g in range(PASSES1):
                     reorder_w2(s * PASSES1 + g)
             if live(s + AHEAD):

from contextlib import ExitStack

import concourse.mybir as mybir
from concourse.masks import make_identity

F32 = mybir.dt.float32
BF16 = mybir.dt.bfloat16
I32 = mybir.dt.int32
U32 = mybir.dt.uint32
U8 = mybir.dt.uint8
FP8X4 = mybir.dt.float8_e4m3fn_x4
ADD = mybir.AluOpType.add
MULT = mybir.AluOpType.mult
RELU = mybir.ActivationFunctionType.Relu

TREES, BATCH, D_H, D_K, D_OUT = 2, 4096, 1024, 512, 256
P = 128
PACK = 4
K_PASS = P * PACK
PASSES1 = D_H // K_PASS
PLANES = 2
WORDS_PASS = K_PASS // 2
ROUNDS = BATCH // P
CHUNK = 4
UNIT_ROWS = CHUNK * P
CHUNKS = ROUNDS // CHUNK
UNITS = CHUNKS * TREES
HALF = CHUNK // 2
QUADRANT = 32
SCALE_ROWS = 4
SPLIT = 7
FIRST_SPLIT = 4
FIRST_LAYER_LAG = 2
BUSY_FIRST = 4
BUSY_BETWEEN = 3
RUN = 4
WHOLE_UNIT = slice(0, UNIT_ROWS)
ONE_LOAD = 3
AHEAD = 6

FLOPS = 2 * TREES * BATCH * (D_H * D_K + D_K * D_OUT)


def tile_randomforestmlp_pa_t_e_kernel(
    tc, h1, W2_words, W2_scales, b2, W3_words, W3_scales, b3, out
):
    nc = tc.nc
    h1_rows = [h1[e].rearrange("(p r) k -> p r k", r=ROUNDS) for e in range(TREES)]
    out_rows = out.rearrange("(p r) n -> p r n", r=ROUNDS)

    with ExitStack() as ctx:
        ctx.enter_context(tc.manual_schedule())
        consts = ctx.enter_context(tc.tile_pool(name="consts", bufs=1))
        h1_pool = ctx.enter_context(tc.tile_pool(name="h1_pool", bufs=AHEAD + 1))
        work = ctx.enter_context(tc.tile_pool(name="work", bufs=3))
        psum_h1t = ctx.enter_context(tc.psum_pool(name="psum_h1t", bufs=4))
        psum_acc1 = ctx.enter_context(tc.psum_pool(name="psum_acc1", bufs=4))

        ones = consts.tile([P, P], BF16, name="ones")
        zeros = consts.tile([P, UNIT_ROWS], BF16, name="zeros")
        nc.vector.memset(ones[:], 1.0)
        nc.vector.memset(zeros[:], 0.0)

        ident = consts.tile([P, P], F32, name="ident")
        make_identity(nc, ident[:])

        warm = consts.tile([P, 2], F32, name="warm")
        nc.vector.memset(warm[:], 0.0)
        nc.scalar.activation(out=warm[:, 1:2], in_=warm[:, 0:1], func=RELU)

        w2_planes_raw = consts.tile([P, D_K], U8, name="w2_planes_raw", align_bytes=64)
        w2_planes = consts.tile([P, D_K], U8, name="w2_planes", align_bytes=64)
        w3_planes = consts.tile([P, D_OUT], U8, name="w3_planes", align_bytes=64)
        nc.vector.memset(w2_planes_raw[:].bitcast(I32), 0)
        nc.vector.memset(w3_planes[:].bitcast(I32), 0)
        w2_raw = consts.tile([P, TREES * PASSES1, D_K], U32, name="w2_raw", align_bytes=64)
        w2 = consts.tile([P, TREES * PASSES1, D_K], U32, name="w2", align_bytes=64)
        w3 = consts.tile([P, TREES, D_OUT], U32, name="w3", align_bytes=64)

        b2_cols_bf = consts.tile([P, TREES, PACK], BF16, name="b2_cols_bf")
        b2_cols = consts.tile([P, TREES, PACK], F32, name="b2_cols")
        nc.scalar.dma_start(out=b2_cols_bf[:], in_=b2.rearrange("e (p t) -> p e t", t=PACK))

        b3_rows = consts.tile([P, HALF, D_OUT], BF16, name="b3_rows")
        nc.vector.memset(b3_rows[:], 0.0)
        for j in range(HALF):
            nc.scalar.dma_start(out=b3_rows[0:TREES, j, :], in_=b3)
        b3_half = consts.tile([P, HALF, D_OUT], F32, name="b3_half")
        nc.vector.tensor_copy(out=b2_cols[:], in_=b2_cols_bf[:])

        h1_sb = {}

        def load_h1(n, rounds=range(CHUNK)):
            c, e = divmod(n, TREES)
            if n not in h1_sb:
                h1_sb[n] = h1_pool.tile([P, CHUNK * D_H], BF16, name="h1_sb")
            x = h1_sb[n]
            if n >= ONE_LOAD:
                nc.sync.dma_start(
                    out=x[:],
                    in_=h1_rows[e][:, CHUNK * c : CHUNK * (c + 1), :].rearrange("p r k -> p (r k)"),
                )
                return
            for i in rounds:
                nc.sync.dma_start(
                    out=x[:, i * D_H : (i + 1) * D_H], in_=h1_rows[e][:, CHUNK * c + i, :]
                )

        def load_planes(planes_sb, scales):
            passes = scales.shape[0]
            for q in range(P // QUADRANT):
                first = QUADRANT * q
                nc.sync.dma_start(
                    out=planes_sb[first : first + SCALE_ROWS * passes, :].bitcast(I32),
                    in_=scales[:, SCALE_ROWS * q : SCALE_ROWS * (q + 1), :].bitcast(I32),
                )

        def load_words(words_sb, words, g):
            nc.sync.dma_start(
                out=words_sb[:, g, :].bitcast(I32),
                in_=words[g].rearrange("p n t -> p (n t)").bitcast(I32),
            )

        load_h1(0)
        load_h1(1)
        load_planes(w2_planes_raw, W2_scales)
        load_words(w2_raw, W2_words, 0)
        load_words(w2_raw, W2_words, 1)
        load_h1(2)
        load_words(w2_raw, W2_words, 2)
        load_words(w2_raw, W2_words, 3)
        load_h1(3)
        load_h1(4)
        load_planes(w3_planes, W3_scales)
        load_words(w3, W3_words, 0)
        load_words(w3, W3_words, 1)
        for n in range(5, AHEAD):
            load_h1(n)

        def reorder_w2_planes():
            nc.vector.tensor_copy(
                out=w2_planes[:].rearrange("p (t m) -> p m t", t=PACK),
                in_=w2_planes_raw[:].rearrange("p (m t) -> p m t", t=PACK),
            )

        def reorder_w2(w):
            nc.vector.tensor_copy(
                out=w2[:, w, :].bitcast(I32).rearrange("p (t m) -> p t m", t=PACK),
                in_=w2_raw[:, w, :].bitcast(I32).rearrange("p (m t) -> p t m", t=PACK),
            )

        def keep_busy(count):
            for i in range(count):
                unread = psum_acc1.tile([P, UNIT_ROWS], F32, name="acc1")
                nc.tensor.matmul(out=unread[:], lhsT=ones[:], rhs=zeros[:], start=True, stop=True)

        def spread_b3():
            spread = psum_acc1.tile([P, HALF, D_OUT], F32, name="acc1")
            nc.tensor.matmul(
                out=spread[:].rearrange("p j n -> p (j n)"),
                lhsT=ones[:],
                rhs=b3_rows[:].rearrange("p j n -> p (j n)"),
                start=True, stop=True,
            )
            nc.scalar.mul(out=b3_half[:], in_=spread[:], mul=1.0 / TREES)

        h1_planes, h1_grouped, h1_q = {}, {}, {}
        h2_slots, h2_grouped, h2_q = {}, {}, {}
        acc2 = {}

        def split_planes(n):
            planes = work.tile([P, PLANES, SPLIT, P], F32, name="h1_planes")
            nc.vector.tensor_copy(
                out=planes[:],
                in_=h1_sb[n][:, 0 : SPLIT * K_PASS]
                .bitcast(F32)
                .rearrange("p (a m u) -> p u a m", m=P, u=PLANES),
            )
            h1_planes[n] = planes

        def transpose_h1(n, rounds):
            if n not in h1_grouped:
                h1_grouped[n] = work.tile(
                    [P, PASSES1, CHUNK, P, PACK], BF16, name="h1_grouped", align_bytes=64
                )
            grouped = h1_grouped[n]
            for i in rounds:
                words = h1_sb[n][:, i * D_H : (i + 1) * D_H].bitcast(F32)
                bank = psum_h1t.tile([P, PASSES1, PLANES, P], F32, name="h1t")
                for g in range(PASSES1):
                    for u in range(PLANES):
                        if n in h1_planes and i * PASSES1 + g < SPLIT:
                            plane = h1_planes[n][:, u, i * PASSES1 + g, :]
                        else:
                            plane = words[:, WORDS_PASS * g + u : WORDS_PASS * (g + 1) : PLANES]
                        nc.tensor.transpose(bank[:, g, u, :], plane, ident[:])
                nc.scalar.copy(
                    out=grouped[:, :, i].bitcast(F32),
                    in_=bank[:].rearrange("p g u b -> p g b u"),
                )

        def quantise_h1(n, rows=WHOLE_UNIT):
            if n not in h1_q:
                h1_q[n] = (
                    work.tile([P, PASSES1 * UNIT_ROWS], U32, name="h1_codes", align_bytes=64),
                    work.tile([P, PASSES1 * UNIT_ROWS], U8, name="h1_scales", align_bytes=64),
                )
            codes, scales = h1_q[n]
            if rows == WHOLE_UNIT:
                nc.vector.quantize_mx(
                    out=codes[:].bitcast(FP8X4),
                    scales=scales[:],
                    in_=h1_grouped[n][:].rearrange("p g i b t -> p (g i b t)"),
                )
                return
            rounds = slice(rows.start // P, rows.stop // P)
            for g in range(PASSES1):
                cols = slice(g * UNIT_ROWS + rows.start, g * UNIT_ROWS + rows.stop)
                nc.vector.quantize_mx(
                    out=codes[:, cols].bitcast(FP8X4),
                    scales=scales[:, cols],
                    in_=h1_grouped[n][:, g, rounds].rearrange("p i b t -> p (i b t)"),
                )

        def first_layer(n, slot_range, rows=WHOLE_UNIT, pool=psum_acc1, tag="acc1"):
            e = n % TREES
            codes, scales = h1_q[n]
            if n not in h2_slots:
                h2_slots[n] = work.tile([P, PACK, UNIT_ROWS], BF16, name="h2_slots")
            slots = h2_slots[n]
            for t in slot_range:
                sums = pool.tile([P, rows.stop - rows.start], F32, name=tag)
                chans = slice(t * P, (t + 1) * P)
                for g in range(PASSES1):
                    w = e * PASSES1 + g
                    cols = slice(g * UNIT_ROWS + rows.start, g * UNIT_ROWS + rows.stop)
                    nc.tensor.matmul_mx(
                        out=sums[:],
                        lhsT=w2[:, w, chans].bitcast(FP8X4),
                        lhsT_scale=w2_planes[SCALE_ROWS * w : P, chans],
                        rhs=codes[:, cols].bitcast(FP8X4),
                        rhs_scale=scales[:, cols],
                        start=(g == 0),
                        stop=(g == PASSES1 - 1),
                    )
                nc.scalar.activation(
                    out=slots[:, t, rows], in_=sums[:], func=RELU, bias=b2_cols[:, e, t : t + 1]
                )

        def regroup_h2(n, rows=WHOLE_UNIT, copy=nc.vector.tensor_copy):
            if n not in h2_grouped:
                h2_grouped[n] = work.tile(
                    [P, UNIT_ROWS, PACK], BF16, name="h2_grouped", align_bytes=64
                )
            copy(
                out=h2_grouped[n][:, rows, :].rearrange("p (c i) t -> p c t i", i=RUN),
                in_=h2_slots[n][:, :, rows].rearrange("p t (c i) -> p c t i", i=RUN),
            )

        def quantise_h2(n, rows=WHOLE_UNIT):
            if n not in h2_q:
                h2_q[n] = (
                    work.tile([P, UNIT_ROWS], U32, name="h2_codes", bufs=5, align_bytes=64),
                    work.tile([P, UNIT_ROWS], U8, name="h2_scales", bufs=5, align_bytes=64),
                )
            codes, scales = h2_q[n]
            nc.vector.quantize_mx(
                out=codes[:, rows].bitcast(FP8X4),
                scales=scales[:, rows],
                in_=h2_grouped[n][:, rows, :].rearrange("p b t -> p (b t)"),
            )

        def second_layer(c, j, pool, tag):
            bank = pool.tile([P, HALF, D_OUT], F32, name=tag)
            for ii in range(HALF):
                cols = slice((HALF * j + ii) * P, (HALF * j + ii + 1) * P)
                for e in range(TREES):
                    codes, scales = h2_q[TREES * c + e]
                    nc.tensor.matmul_mx(
                        out=bank[:, ii, :],
                        lhsT=codes[:, cols].bitcast(FP8X4),
                        lhsT_scale=scales[:, cols],
                        rhs=w3[:, e, :].bitcast(FP8X4),
                        rhs_scale=w3_planes[SCALE_ROWS * e : P, :],
                        start=(e == 0),
                        stop=(e == TREES - 1),
                    )
            acc2[(c, j)] = bank

        def finish(c, j):
            result = work.tile([P, HALF, D_OUT], F32, name="result", bufs=6)
            nc.vector.scalar_tensor_tensor(
                out=result[:], in0=acc2[(c, j)][:],
                scalar=1.0 / TREES, in1=b3_half[:], op0=MULT, op1=ADD,
            )
            first = CHUNK * c + HALF * j
            nc.sync.dma_start(out=out_rows[:, first : first + HALF, :], in_=result[:])

        def live(n):
            return 0 <= n < UNITS

        halves = [slice(j * HALF * P, (j + 1) * HALF * P) for j in range(CHUNK // HALF)]

        def step(s):
            if live(s - 5):
                finish(*divmod(s - 5, 2))
            if live(s + 1) and s + 1 >= FIRST_SPLIT:
                split_planes(s + 1)
            if live(s - 2):
                regroup_h2(s - 2)
            transpose_h1(s, range(CHUNK))
            if s == 0:
                keep_busy(2)
                spread_b3()
            if live(s - 1):
                first_layer(s - 1, range(PACK))
            if live(s - 4):
                second_layer(*divmod(s - 4, 2), psum_acc1, "acc1")
            if s == 0:
                for rows in halves:
                    quantise_h1(s, rows)
                reorder_w2_planes()
                reorder_w2(0)
                reorder_w2(1)
            elif s < UNITS - 1:
                quantise_h1(s)
            else:
                for rows in halves:
                    quantise_h1(s, rows)
            if live(s - 2):
                quantise_h2(s - 2)
            if s == 1:
                for g in range(PASSES1):
                    reorder_w2(s * PASSES1 + g)
            if live(s + AHEAD):
                load_h1(s + AHEAD)

        keep_busy(BUSY_FIRST)
        for s in range(UNITS):
            step(s)

        last = UNITS - 1
        end_c = CHUNKS - 1
        finish(end_c - 2, 1)
        first_layer(last, range(PACK), halves[0], psum_h1t, "h1t")
        first_layer(last, range(PACK), halves[1])
        second_layer(end_c - 1, 0, psum_h1t, "h1t")
        second_layer(end_c - 1, 1, psum_h1t, "h1t")
        regroup_h2(last - 1)
        regroup_h2(last, halves[0])
        regroup_h2(last, halves[1], nc.scalar.copy)
        quantise_h2(last - 1)
        quantise_h2(last, halves[0])
        second_layer(end_c, 0, psum_h1t, "h1t")
        finish(end_c - 1, 0)
        quantise_h2(last, halves[1])
        second_layer(end_c, 1, psum_h1t, "h1t")
        finish(end_c - 1, 1)
        for j in range(CHUNK // HALF):
            finish(end_c, j)
